import numpy as np
import ml_dtypes


def mxq(x, axis, fmt="e4m3"):
    dtype, down = {"e4m3": (ml_dtypes.float8_e4m3fn, 7), "e5m2": (ml_dtypes.float8_e5m2, 14)}[fmt]
    v = np.moveaxis(np.asarray(x, np.float32).astype(ml_dtypes.bfloat16).astype(np.float64), axis, -1)
    blocks = v.reshape(v.shape[:-1] + (-1, 32))
    amax = np.abs(blocks).max(-1, keepdims=True)
    byte = np.maximum(np.where(amax > 0, np.frexp(amax)[1] - 1 + 127, 0) - down, 1)
    scale = np.exp2(byte - 127.0)
    codes = (blocks / scale).astype(np.float32).astype(dtype).astype(np.float64)
    return np.moveaxis((codes * scale).reshape(v.shape), -1, axis)


WIDE = False


def mx_kscale(k):
    if not WIDE:
        return np.ones(k)
    levels = np.array([10, -10, 5, -5, 0])
    a = np.random.permutation(np.resize(levels, k // 512 * 4)).reshape(k // 512, 4)
    idx = np.arange(k)
    return np.exp2(a[idx // 512, idx % 128 // 32])


BF16 = ml_dtypes.bfloat16


def bf(x):
    return np.asarray(x, np.float32).astype(BF16)


def f64(x):
    return np.asarray(x).astype(np.float64)


B, N, D, P, C = 2, 512, 1024, 32, 5
G = 11 + C
O = P * G
OFFSET_MAX = 0.2
SCALE_MAX = 0.02


def sigmoid(v):
    return 1.0 / (1.0 + np.exp(-v))


def silu(v):
    return v / (1.0 + np.exp(-v))


def setup_inputs():
    s = mx_kscale(D)
    return {"xyzs": bf(np.random.standard_normal((B, N, 3)) * 0.25),
            "latents": bf(np.random.standard_normal((B, N, D)) * s),
            "W1": bf(np.random.standard_normal((D, O)) / np.sqrt(D) / s[:, None]),
            "b1": bf(np.random.standard_normal(O) * 0.3),
            "W2": bf(np.random.standard_normal((O, O)) * 2.5 / np.sqrt(O)),
            "b2": bf(np.random.standard_normal(O) * 0.5)}


def reference(xyzs, latents, W1, b1, W2, b2):
    xyzs = f64(xyzs)
    h = silu((mxq(f64(latents), 2, "e4m3") @ mxq(f64(W1), 0, "e4m3")) + f64(b1))
    f = (mxq(h, 2, "e4m3") @ mxq(f64(W2), 0, "e4m3")) + f64(b2)
    f = f.reshape(B, N, P, G)
    mean3D = xyzs[:, :, None, :] + sigmoid(f[..., 0:3]) * OFFSET_MAX
    opacity = sigmoid(f[..., 3:4])
    scales = sigmoid(f[..., 4:7]) * SCALE_MAX
    rot = f[..., 7:11]
    rot = rot / np.maximum(np.sqrt(np.sum(rot * rot, axis=-1, keepdims=True)), 1e-12)
    rgb = np.clip(f[..., 11:], -0.5, 0.5) + 0.5
    gaussians = np.concatenate([mean3D, opacity, scales, rot, rgb], axis=-1)
    return gaussians.reshape(B, N * P, G)

@@ -1,0 +1,222 @@
+from contextlib import ExitStack
+
+import concourse.mybir as mybir
+from concourse.masks import make_identity
+
+FP8X4 = mybir.dt.float8_e4m3fn_x4
+BF16 = mybir.dt.bfloat16
+F32 = mybir.dt.float32
+U32 = mybir.dt.uint32
+U8 = mybir.dt.uint8
+ACT = mybir.ActivationFunctionType
+ALU = mybir.AluOpType
+AX = mybir.AxisListType
+
+P = 128
+TOK = 1024
+D = 1024
+O = 512
+NT = TOK // P
+G = 16
+NG = O // G
+
+FLOPS = 2 * TOK * D * O + 2 * TOK * O * O
+
+
+def regroup(nc, dst, src):
+    nc.vector.tensor_copy(
+        out=dst.rearrange("p (c i) t -> p c t i", i=4),
+        in_=src.rearrange("p t (c i) -> p c t i", i=4),
+    )
+
+
+def tile_gaussianrenderer_kernel(tc, xyzs, latents, W1, b1, W2, b2, out):
+    nc = tc.nc
+    lat_v = latents.rearrange("b n d -> (b n) d").rearrange("(p i) d -> p i d", i=NT)
+    xyz_v = xyzs.rearrange("b n c -> (b n) c").rearrange("(p i) c -> p i c", i=NT)
+    out_v = out.rearrange("b (n g) c -> (b n) (g c)", g=NG).rearrange("(p i) f -> p i f", i=NT)
+    w1_v = W1.rearrange("(a q e) c -> q a (e c)", a=4, e=2)
+    w2_v = W2.rearrange("(t p) n -> p t n", p=P)
+
+    with ExitStack() as ctx:
+        keep = ctx.enter_context(tc.tile_pool(name="keep", bufs=1))
+        stage = ctx.enter_context(tc.tile_pool(name="stage", bufs=2))
+        psum = ctx.enter_context(tc.psum_pool(name="psum", bufs=8))
+
+        warm = keep.tile([P, 1], F32)
+        nc.vector.memset(warm[:], 0.0)
+        nc.scalar.activation(out=warm[:], in_=warm[:], func=ACT.Silu)
+        ident = keep.tile([P, P], F32)
+        make_identity(nc, ident[:])
+        zb = keep.tile([P, O], BF16)
+        nc.vector.memset(zb[:], 0.0)
+        ones = keep.tile([P, P], BF16)
+        nc.vector.memset(ones[:], 1.0)
+        s4 = keep.tile([P, 4], F32)
+        nc.vector.memset(s4[:], 0.01)
+        nc.vector.memset(s4[:, 0:1], 0.5)
+
+        nc.scalar.dma_start(out=zb[0:1, :], in_=b2.unsqueeze(0))
+        b1_sb = keep.tile([P, 4], BF16)
+        with nc.allow_non_contiguous_dma(reason="512 bias values, one to a partition and group"):
+            nc.scalar.dma_start(out=b1_sb[:], in_=b1.rearrange("(m p) -> p m", p=P))
+        xyz_sb = keep.tile([P, NT, 3], BF16)
+        nc.scalar.dma_start(out=xyz_sb[:], in_=xyz_v)
+
+        w1r = keep.tile([P, 4, 2 * O], BF16)
+        x_sb = keep.tile([P, NT, D], BF16)
+        w2r = keep.tile([P, 4, O], BF16)
+        for g in range(2):
+            nc.sync.dma_start(out=w1r[:, 2 * g : 2 * g + 2, :], in_=w1_v[:, 2 * g : 2 * g + 2, :])
+        for h in range(4):
+            nc.sync.dma_start(out=x_sb[:, 2 * h : 2 * h + 2, :], in_=lat_v[:, 2 * h : 2 * h + 2, :])
+        nc.sync.dma_start(out=w2r[:], in_=w2_v)
+
+        pb = psum.tile([P, O], F32, tag="bank", name="pb")
+        nc.tensor.matmul(out=pb[:], lhsT=ones[:], rhs=zb[:], start=True, stop=True)
+        b2bc = keep.tile([P, NG, G], F32)
+        nc.vector.tensor_copy(out=b2bc[:].rearrange("p g c -> p (g c)"), in_=pb[:])
+        nc.vector.tensor_scalar_add(out=b2bc[:, :, 11:16], in0=b2bc[:, :, 11:16], scalar1=0.5)
+        b1f = keep.tile([P, 4], F32)
+        nc.vector.tensor_copy(out=b1f[:], in_=b1_sb[:])
+        a3 = keep.tile([P, NT, 3], F32)
+        nc.vector.tensor_scalar_add(out=a3[:], in0=xyz_sb[:], scalar1=0.1)
+
+        w1c = keep.tile([P, 2, O], U32, align_bytes=64)
+        w1s = keep.tile([P, 2, O], U8, align_bytes=64)
+        w1g = []
+        for g in range(2):
+            wg = keep.tile([P, O, 4], BF16, align_bytes=64, name="w1g%d" % g)
+            src = w1r[:, 2 * g : 2 * g + 2, :].rearrange("p u (e c) -> p (u e) c", e=2)
+            regroup(nc, wg[:], src)
+            w1g.append(wg)
+        for g in range(2):
+            nc.vector.quantize_mx(
+                out=w1c[:, g, :].bitcast(FP8X4),
+                scales=w1s[:, g, :],
+                in_=w1g[g][:].rearrange("p c t -> p (c t)"),
+            )
+
+        lc = keep.tile([P, 2, TOK], U32, align_bytes=64)
+        ls = keep.tile([P, 2, TOK], U8, align_bytes=64)
+        hc = keep.tile([P, TOK], U32, align_bytes=64)
+        hs = keep.tile([P, TOK], U8, align_bytes=64)
+        w2c = keep.tile([P, O], U32, align_bytes=64)
+        w2s = keep.tile([P, O], U8, align_bytes=64)
+        hps = []
+
+        for c in range(2):
+            cols = slice(c * 512, c * 512 + 512)
+            lgs = []
+            for g in range(2):
+                lg = stage.tile([P, 2048], BF16, align_bytes=64, tag="lg", bufs=4, name="lg%d%d" % (c, g))
+                lgs.append(lg)
+            for h in range(2):
+                for g in range(2):
+                    xt = psum.tile([P, 512], F32, tag="bank", name="xt%d%d%d" % (c, h, g))
+                    xt_v = xt[:].rearrange("p (u t) -> p u t", u=2)
+                    for il in range(2):
+                        i = 4 * c + 2 * h + il
+                        x32 = x_sb[:, i, :].bitcast(F32)
+                        for u in range(2):
+                            w0 = 256 * g + 128 * u
+                            nc.tensor.transpose(
+                                out=xt_v[:, u, il * P : il * P + P],
+                                in_=x32[:, w0 : w0 + P],
+                                identity=ident[:],
+                            )
+                    lg32 = lgs[g][:].bitcast(F32).rearrange("p (t u) -> p t u", u=2)
+                    nc.scalar.copy(
+                        out=lg32[:, 256 * h : 256 * h + 256, :],
+                        in_=xt_v.rearrange("p u t -> p t u"),
+                    )
+            for g in range(2):
+                nc.vector.quantize_mx(
+                    out=lc[:, g, cols].bitcast(FP8X4), scales=ls[:, g, cols], in_=lgs[g][:]
+                )
+            hp = stage.tile([P, 4, 512], BF16, tag="hp", name="hp%d" % c)
+            hps.append(hp)
+            for m in range(4):
+                mc = slice(m * P, m * P + P)
+                ps = psum.tile([P, 512], F32, tag="bank", name="l1_%d%d" % (c, m))
+                for g in range(2):
+                    nc.tensor.matmul_mx(
+                        out=ps[:],
+                        lhsT=w1c[:, g, mc].bitcast(FP8X4),
+                        lhsT_scale=w1s[:, g, mc],
+                        rhs=lc[:, g, cols].bitcast(FP8X4),
+                        rhs_scale=ls[:, g, cols],
+                        start=(g == 0),
+                        stop=(g == 1),
+                    )
+                nc.scalar.activation(
+                    out=hp[:, m, :], in_=ps[:], func=ACT.Silu, bias=b1f[:, m : m + 1], scale=1.0
+                )
+
+        w2g = keep.tile([P, O, 4], BF16, align_bytes=64)
+        regroup(nc, w2g[:], w2r[:])
+
+        hgs = []
+        for c in range(2):
+            hg = stage.tile([P, 512, 4], BF16, align_bytes=64, tag="hg", name="hg%d" % c)
+            regroup(nc, hg[:], hps[c][:])
+            hgs.append(hg)
+            if c == 0:
+                nc.vector.quantize_mx(
+                    out=w2c[:].bitcast(FP8X4), scales=w2s[:], in_=w2g[:].rearrange("p c t -> p (c t)")
+                )
+            cols = slice(c * 512, c * 512 + 512)
+            nc.vector.quantize_mx(
+                out=hc[:, cols].bitcast(FP8X4), scales=hs[:, cols], in_=hg[:].rearrange("p c t -> p (c t)")
+            )
+
+        o_sb = keep.tile([P, NT, NG, G], F32)
+        sq = keep.tile([P, NT, NG, 4], F32)
+        ss = keep.tile([P, NT, NG], F32)
+        nrm = keep.tile([P, NT, NG], F32)
+        rn = keep.tile([P, NT, NG], F32)
+        for i in range(NT):
+            tcols = slice(i * P, i * P + P)
+            pf = psum.tile([P, 512], F32, tag="bank", name="l2_%d" % i)
+            nc.tensor.matmul_mx(
+                out=pf[:],
+                lhsT=hc[:, tcols].bitcast(FP8X4),
+                lhsT_scale=hs[:, tcols],
+                rhs=w2c[:].bitcast(FP8X4),
+                rhs_scale=w2s[:],
+                start=True,
+                stop=True,
+            )
+            nc.vector.tensor_tensor(
+                out=o_sb[:, i].rearrange("p g c -> p (g c)"),
+                in0=pf[:],
+                in1=b2bc[:].rearrange("p g c -> p (g c)"),
+                op=ALU.add,
+            )
+            nc.scalar.activation(out=o_sb[:, i, :, 0:7], in_=o_sb[:, i, :, 0:7], func=ACT.Tanh, scale=0.5)
+            nc.scalar.activation(out=sq[:, i], in_=o_sb[:, i, :, 7:11], func=ACT.Square)
+            nc.vector.tensor_reduce(out=ss[:, i, :], in_=sq[:, i], axis=AX.X, op=ALU.add)
+            nc.vector.tensor_scalar(
+                out=o_sb[:, i, :, 11:16], in0=o_sb[:, i, :, 11:16],
+                scalar1=0.0, scalar2=1.0, op0=ALU.max, op1=ALU.min,
+            )
+            nc.vector.scalar_tensor_tensor(
+                out=o_sb[:, i, :, 0:3], in0=o_sb[:, i, :, 0:3], scalar=0.1,
+                in1=a3[:, i, :].unsqueeze(1).to_broadcast([P, NG, 3]),
+                op0=ALU.mult, op1=ALU.add,
+            )
+            nc.vector.scalar_tensor_tensor(
+                out=o_sb[:, i, :, 3:7], in0=o_sb[:, i, :, 3:7], scalar=1.0,
+                in1=s4[:].unsqueeze(1).to_broadcast([P, NG, 4]),
+                op0=ALU.add, op1=ALU.mult,
+            )
+        nc.vector.tensor_scalar_max(out=ss[:], in0=ss[:], scalar1=1e-24)
+        nc.scalar.activation(out=nrm[:], in_=ss[:], func=ACT.Sqrt)
+        nc.vector.reciprocal(out=rn[:], in_=nrm[:])
+        for i in range(NT):
+            nc.vector.tensor_tensor(
+                out=o_sb[:, i, :, 7:11], in0=o_sb[:, i, :, 7:11],
+                in1=rn[:, i, :].unsqueeze(2).to_broadcast([P, NG, 4]),
+                op=ALU.mult,
+            )
+            nc.sync.dma_start(out=out_v[:, i, :], in_=o_sb[:, i].rearrange("p g c -> p (g c)"))

@@ -16,17 +16,24 @@ P = 128
 TOK = 1024
 D = 1024
 O = 512
-NT = TOK // P
+NT = 8
 G = 16
-NG = O // G
+NG = 32
+NCH = 4
+CT = 256
+SHIFT = 1
+VCOLS = 384
+CP_ON_VECTOR = []
 
 FLOPS = 2 * TOK * D * O + 2 * TOK * O * O
 
+ORDER = [["rgW1v",0],["rgW1s",0],["qW1",0],["rgW1s",1],["b2c"],["rgW1v",1],["tr",0,0],["qW1",1],["tr",0,1],["cp",0,0],["tr",1,0],["cp",0,1],["tr",1,1],["cp",1,0],["ql",0],["cp",1,1],["rgW2"],["l1",0,0],["l1",0,1],["l1",0,2],["si",0,0],["ql",1],["l1",0,3],["si",0,1],["tr",2,0],["si",0,2],["qW2"],["tr",2,1],["si",0,3],["cp",2,0],["rg",0],["l1",1,0],["l1",1,1],["cp",2,1],["qh",0],["l1",1,2],["l1",1,3],["si",1,0],["ql",2],["tr",3,0],["si",1,1],["tr",3,1],["si",1,2],["l2",0,0],["si",1,3],["l2",0,1],["cp",3,0],["l1",2,0],["A",0,0],["cp",3,1],["l1",2,1],["rg",1],["l1",2,2],["l1",2,3],["si",2,0],["qh",1],["si",2,1],["A",0,1],["si",2,2],["l2",1,0],["si",2,3],["ql",3],["l2",1,1],["sq",0],["th",0],["red",0],["l1",3,0],["clip",0],["C",0],["l1",3,1],["l1",3,2],["si",3,0],["D",0],["l1",3,3],["si",3,1],["A",1,0],["si",3,2],["A",1,1],["si",3,3],["rg",2],["sq",1],["th",1],["qh",2],["red",1],["l2",2,0],["clamp",0],["clip",1],["l2",2,1],["C",1],["D",1],["rg",3],["sqrt",0],["qh",3],["A",2,0],["A",2,1],["l2",3,0],["rcp",0],["th",2],["l2",3,1],["J",0],["J",1],["st",0],["sq",2],["clip",2],["A",3,0],["A",3,1],["st",1],["clip",3],["th",3],["C",2],["sq",3],["D",2],["red",2],["C",3],["D",3],["red",3],["clamp",1],["sqrt",1],["rcp",1],["J",2],["J",3],["st",2],["st",3]]
 
-def regroup(nc, dst, src):
-    nc.vector.tensor_copy(
-        out=dst.rearrange("p (c i) t -> p c t i", i=4),
-        in_=src.rearrange("p t (c i) -> p c t i", i=4),
+
+def runs4(dst, src):
+    return (
+        dst.rearrange("p (c i) t -> p c t i", i=4),
+        src.rearrange("p t (c i) -> p c t i", i=4),
     )
 
 
@@ -39,184 +46,240 @@ def tile_gaussianrenderer_kernel(tc, xyzs, latents, W1, b1, W2, b2, out):
     w2_v = W2.rearrange("(t p) n -> p t n", p=P)
 
     with ExitStack() as ctx:
+        ctx.enter_context(tc.manual_schedule())
         keep = ctx.enter_context(tc.tile_pool(name="keep", bufs=1))
-        stage = ctx.enter_context(tc.tile_pool(name="stage", bufs=2))
-        psum = ctx.enter_context(tc.psum_pool(name="psum", bufs=8))
+        psum = ctx.enter_context(tc.psum_pool(name="psum", bufs=2))
 
         warm = keep.tile([P, 1], F32)
         nc.vector.memset(warm[:], 0.0)
         nc.scalar.activation(out=warm[:], in_=warm[:], func=ACT.Silu)
-        ident = keep.tile([P, P], F32)
-        make_identity(nc, ident[:])
         zb = keep.tile([P, O], BF16)
         nc.vector.memset(zb[:], 0.0)
         ones = keep.tile([P, P], BF16)
         nc.vector.memset(ones[:], 1.0)
-        s4 = keep.tile([P, 4], F32)
-        nc.vector.memset(s4[:], 0.01)
-        nc.vector.memset(s4[:, 0:1], 0.5)
+        ident = keep.tile([P, P], F32)
+        make_identity(nc, ident[:])
 
-        nc.scalar.dma_start(out=zb[0:1, :], in_=b2.unsqueeze(0))
+        xyz_sb = keep.tile([P, NT, 3], BF16)
+        nc.scalar.dma_start(out=xyz_sb[:], in_=xyz_v)
         b1_sb = keep.tile([P, 4], BF16)
         with nc.allow_non_contiguous_dma(reason="512 bias values, one to a partition and group"):
             nc.scalar.dma_start(out=b1_sb[:], in_=b1.rearrange("(m p) -> p m", p=P))
-        xyz_sb = keep.tile([P, NT, 3], BF16)
-        nc.scalar.dma_start(out=xyz_sb[:], in_=xyz_v)
+        nc.scalar.dma_start(out=zb[0:1, :], in_=b2.unsqueeze(0))
 
         w1r = keep.tile([P, 4, 2 * O], BF16)
         x_sb = keep.tile([P, NT, D], BF16)
         w2r = keep.tile([P, 4, O], BF16)
-        for g in range(2):
-            nc.sync.dma_start(out=w1r[:, 2 * g : 2 * g + 2, :], in_=w1_v[:, 2 * g : 2 * g + 2, :])
-        for h in range(4):
-            nc.sync.dma_start(out=x_sb[:, 2 * h : 2 * h + 2, :], in_=lat_v[:, 2 * h : 2 * h + 2, :])
-        nc.sync.dma_start(out=w2r[:], in_=w2_v)
 
-        pb = psum.tile([P, O], F32, tag="bank", name="pb")
+        def load(what, j):
+            if what == "W1":
+                nc.sync.dma_start(out=w1r[:, 2 * j : 2 * j + 2, :], in_=w1_v[:, 2 * j : 2 * j + 2, :])
+            elif what == "L":
+                nc.sync.dma_start(out=x_sb[:, 2 * j : 2 * j + 2, :], in_=lat_v[:, 2 * j : 2 * j + 2, :])
+            else:
+                nc.sync.dma_start(out=w2r[:], in_=w2_v)
+
+        for what, j in (("W1", 0), ("W1", 1), ("L", 0), ("L", 1), ("W2", 0), ("L", 2), ("L", 3)):
+            load(what, j)
+
+        s4 = keep.tile([P, 4], F32)
+        nc.gpsimd.memset(s4[:], 1.0)
+        nc.gpsimd.tensor_scalar(out=s4[:, 0:1], in0=s4[:, 0:1], scalar1=0.5, scalar2=0.0, op0=ALU.mult, op1=ALU.add)
+        nc.gpsimd.tensor_scalar(out=s4[:, 1:4], in0=s4[:, 1:4], scalar1=0.01, scalar2=0.0, op0=ALU.mult, op1=ALU.add)
+        a3x = keep.tile([P, NT, NG, 3], F32)
+        nc.gpsimd.tensor_scalar(
+            out=a3x[:], in0=xyz_sb[:].unsqueeze(2).to_broadcast([P, NT, NG, 3]),
+            scalar1=1.0, scalar2=0.1, op0=ALU.mult, op1=ALU.add,
+        )
+        b1f = keep.tile([P, 4], F32)
+        nc.gpsimd.tensor_scalar(out=b1f[:], in0=b1_sb[:], scalar1=1.0, scalar2=0.0, op0=ALU.mult, op1=ALU.add)
+        pb = psum.tile([P, O], F32, tag="l2", name="pb")
         nc.tensor.matmul(out=pb[:], lhsT=ones[:], rhs=zb[:], start=True, stop=True)
         b2bc = keep.tile([P, NG, G], F32)
-        nc.vector.tensor_copy(out=b2bc[:].rearrange("p g c -> p (g c)"), in_=pb[:])
-        nc.vector.tensor_scalar_add(out=b2bc[:, :, 11:16], in0=b2bc[:, :, 11:16], scalar1=0.5)
-        b1f = keep.tile([P, 4], F32)
-        nc.vector.tensor_copy(out=b1f[:], in_=b1_sb[:])
-        a3 = keep.tile([P, NT, 3], F32)
-        nc.vector.tensor_scalar_add(out=a3[:], in0=xyz_sb[:], scalar1=0.1)
 
+        def b2c():
+            nc.scalar.copy(out=b2bc[:].rearrange("p g c -> p (g c)"), in_=pb[:])
+            nc.gpsimd.tensor_scalar(
+                out=b2bc[:, :, 11:16], in0=b2bc[:, :, 11:16], scalar1=1.0, scalar2=0.5, op0=ALU.mult, op1=ALU.add
+            )
+
+        w1g = [keep.tile([P, O, 4], BF16, align_bytes=64, name="w1g%d" % g) for g in range(2)]
         w1c = keep.tile([P, 2, O], U32, align_bytes=64)
         w1s = keep.tile([P, 2, O], U8, align_bytes=64)
-        w1g = []
-        for g in range(2):
-            wg = keep.tile([P, O, 4], BF16, align_bytes=64, name="w1g%d" % g)
-            src = w1r[:, 2 * g : 2 * g + 2, :].rearrange("p u (e c) -> p (u e) c", e=2)
-            regroup(nc, wg[:], src)
-            w1g.append(wg)
-        for g in range(2):
-            nc.vector.quantize_mx(
-                out=w1c[:, g, :].bitcast(FP8X4),
-                scales=w1s[:, g, :],
-                in_=w1g[g][:].rearrange("p c t -> p (c t)"),
-            )
-
-        lc = keep.tile([P, 2, TOK], U32, align_bytes=64)
-        ls = keep.tile([P, 2, TOK], U8, align_bytes=64)
-        hc = keep.tile([P, TOK], U32, align_bytes=64)
-        hs = keep.tile([P, TOK], U8, align_bytes=64)
+        w2g = keep.tile([P, O, 4], BF16, align_bytes=64)
         w2c = keep.tile([P, O], U32, align_bytes=64)
         w2s = keep.tile([P, O], U8, align_bytes=64)
-        hps = []
+        lg = [keep.tile([P, 8 * CT], BF16, align_bytes=64, name="lg%d" % k) for k in range(NCH)]
+        lc = keep.tile([P, NCH, 2 * CT], U32, align_bytes=64)
+        ls = keep.tile([P, NCH, 2 * CT], U8, align_bytes=64)
+        hp = [keep.tile([P, 4, CT], BF16, name="hp%d" % k) for k in range(NCH)]
+        hg = [keep.tile([P, CT, 4], BF16, align_bytes=64, name="hg%d" % k) for k in range(NCH)]
+        hc = keep.tile([P, NCH, CT], U32, align_bytes=64)
+        hs = keep.tile([P, NCH, CT], U8, align_bytes=64)
+        o_sb = keep.tile([P, NT * O + 4], F32)
+        sq = [keep.tile([P, 2 * NG, 4], F32, name="sq%d" % k) for k in range(NCH)]
+        tht = [keep.tile([P, 2 * NG, 7], F32, name="tht%d" % k) for k in range(NCH)]
+        ss = keep.tile([P, NT * NG], F32)
+        nrm = keep.tile([P, NT * NG], F32)
+        rn = keep.tile([P, NT * NG], F32)
+        banks = {}
 
-        for c in range(2):
-            cols = slice(c * 512, c * 512 + 512)
-            lgs = []
-            for g in range(2):
-                lg = stage.tile([P, 2048], BF16, align_bytes=64, tag="lg", bufs=4, name="lg%d%d" % (c, g))
-                lgs.append(lg)
-            for h in range(2):
-                for g in range(2):
-                    xt = psum.tile([P, 512], F32, tag="bank", name="xt%d%d%d" % (c, h, g))
-                    xt_v = xt[:].rearrange("p (u t) -> p u t", u=2)
-                    for il in range(2):
-                        i = 4 * c + 2 * h + il
-                        x32 = x_sb[:, i, :].bitcast(F32)
-                        for u in range(2):
-                            w0 = 256 * g + 128 * u
-                            nc.tensor.transpose(
-                                out=xt_v[:, u, il * P : il * P + P],
-                                in_=x32[:, w0 : w0 + P],
-                                identity=ident[:],
-                            )
-                    lg32 = lgs[g][:].bitcast(F32).rearrange("p (t u) -> p t u", u=2)
-                    nc.scalar.copy(
-                        out=lg32[:, 256 * h : 256 * h + 256, :],
-                        in_=xt_v.rearrange("p u t -> p t u"),
-                    )
-            for g in range(2):
-                nc.vector.quantize_mx(
-                    out=lc[:, g, cols].bitcast(FP8X4), scales=ls[:, g, cols], in_=lgs[g][:]
-                )
-            hp = stage.tile([P, 4, 512], BF16, tag="hp", name="hp%d" % c)
-            hps.append(hp)
-            for m in range(4):
-                mc = slice(m * P, m * P + P)
-                ps = psum.tile([P, 512], F32, tag="bank", name="l1_%d%d" % (c, m))
-                for g in range(2):
-                    nc.tensor.matmul_mx(
-                        out=ps[:],
-                        lhsT=w1c[:, g, mc].bitcast(FP8X4),
-                        lhsT_scale=w1s[:, g, mc],
-                        rhs=lc[:, g, cols].bitcast(FP8X4),
-                        rhs_scale=ls[:, g, cols],
-                        start=(g == 0),
-                        stop=(g == 1),
-                    )
-                nc.scalar.activation(
-                    out=hp[:, m, :], in_=ps[:], func=ACT.Silu, bias=b1f[:, m : m + 1], scale=1.0
-                )
+        def oc(k):
+            return o_sb[:, SHIFT + 2 * O * k : SHIFT + 2 * O * (k + 1)].rearrange("p (q c) -> p q c", c=G)
 
-        w2g = keep.tile([P, O, 4], BF16, align_bytes=64)
-        regroup(nc, w2g[:], w2r[:])
+        def w1src(g):
+            return w1r[:, 2 * g : 2 * g + 2, :].rearrange("p u (e c) -> p (u e) c", e=2)
 
-        hgs = []
-        for c in range(2):
-            hg = stage.tile([P, 512, 4], BF16, align_bytes=64, tag="hg", name="hg%d" % c)
-            regroup(nc, hg[:], hps[c][:])
-            hgs.append(hg)
-            if c == 0:
-                nc.vector.quantize_mx(
-                    out=w2c[:].bitcast(FP8X4), scales=w2s[:], in_=w2g[:].rearrange("p c t -> p (c t)")
-                )
-            cols = slice(c * 512, c * 512 + 512)
+        def rgW1v(g):
+            d, s = runs4(w1g[g][:, 0:VCOLS, :], w1src(g)[:, :, 0:VCOLS])
+            nc.vector.tensor_copy(out=d, in_=s)
+
+        def rgW1s(g):
+            d, s = runs4(w1g[g][:, VCOLS:O, :], w1src(g)[:, :, VCOLS:O])
+            nc.scalar.copy(out=d, in_=s)
+
+        def qW1(g):
             nc.vector.quantize_mx(
-                out=hc[:, cols].bitcast(FP8X4), scales=hs[:, cols], in_=hg[:].rearrange("p c t -> p (c t)")
+                out=w1c[:, g, :].bitcast(FP8X4), scales=w1s[:, g, :], in_=w1g[g][:].rearrange("p c t -> p (c t)")
             )
 
-        o_sb = keep.tile([P, NT, NG, G], F32)
-        sq = keep.tile([P, NT, NG, 4], F32)
-        ss = keep.tile([P, NT, NG], F32)
-        nrm = keep.tile([P, NT, NG], F32)
-        rn = keep.tile([P, NT, NG], F32)
-        for i in range(NT):
-            tcols = slice(i * P, i * P + P)
-            pf = psum.tile([P, 512], F32, tag="bank", name="l2_%d" % i)
+        def rgW2():
+            d, s = runs4(w2g[:], w2r[:])
+            nc.vector.tensor_copy(out=d, in_=s)
+
+        def qW2():
+            nc.vector.quantize_mx(out=w2c[:].bitcast(FP8X4), scales=w2s[:], in_=w2g[:].rearrange("p c t -> p (c t)"))
+
+        def tr(k, g):
+            xt = psum.tile([P, 512], F32, tag="xt", bufs=4, name="xt%d%d" % (k, g))
+            banks[("xt", k, g)] = xt
+            xt_v = xt[:].rearrange("p (u t) -> p u t", u=2)
+            for il in range(2):
+                x32 = x_sb[:, 2 * k + il, :].bitcast(F32)
+                for u in range(2):
+                    w0 = 256 * g + 128 * u
+                    nc.tensor.transpose(
+                        out=xt_v[:, u, il * P : il * P + P], in_=x32[:, w0 : w0 + P], identity=ident[:]
+                    )
+
+        def cp(k, g):
+            xt_v = banks[("xt", k, g)][:].rearrange("p (u t) -> p t u", u=2)
+            dst = lg[k][:].bitcast(F32).rearrange("p (g t u) -> p g t u", g=2, u=2)[:, g]
+            if "%d_%d" % (k, g) in CP_ON_VECTOR:
+                nc.vector.tensor_copy(out=dst, in_=xt_v)
+            else:
+                nc.scalar.copy(out=dst, in_=xt_v)
+
+        def ql(k):
+            nc.vector.quantize_mx(out=lc[:, k, :].bitcast(FP8X4), scales=ls[:, k, :], in_=lg[k][:])
+
+        def l1(k, m):
+            if m % 2 == 0:
+                banks[("l1", k, m // 2)] = psum.tile([P, 512], F32, tag="l1", bufs=2, name="l1_%d%d" % (k, m // 2))
+            ps = banks[("l1", k, m // 2)][:, (m % 2) * CT : (m % 2) * CT + CT]
+            mc = slice(m * P, m * P + P)
+            for g in range(2):
+                tcols = slice(g * CT, g * CT + CT)
+                nc.tensor.matmul_mx(
+                    out=ps,
+                    lhsT=w1c[:, g, mc].bitcast(FP8X4),
+                    lhsT_scale=w1s[:, g, mc],
+                    rhs=lc[:, k, tcols].bitcast(FP8X4),
+                    rhs_scale=ls[:, k, tcols],
+                    start=(g == 0),
+                    stop=(g == 1),
+                )
+
+        def si(k, m):
+            ps = banks[("l1", k, m // 2)][:, (m % 2) * CT : (m % 2) * CT + CT]
+            nc.scalar.activation(out=hp[k][:, m, :], in_=ps, func=ACT.Silu, bias=b1f[:, m : m + 1], scale=1.0)
+
+        def rg(k):
+            d, s = runs4(hg[k][:], hp[k][:])
+            nc.vector.tensor_copy(out=d, in_=s)
+
+        def qh(k):
+            nc.vector.quantize_mx(
+                out=hc[:, k, :].bitcast(FP8X4), scales=hs[:, k, :], in_=hg[k][:].rearrange("p c t -> p (c t)")
+            )
+
+        def l2(k, t):
+            pf = psum.tile([P, 512], F32, tag="l2", bufs=2, name="l2_%d%d" % (k, t))
+            banks[("l2", k, t)] = pf
+            tcols = slice(t * P, t * P + P)
             nc.tensor.matmul_mx(
                 out=pf[:],
-                lhsT=hc[:, tcols].bitcast(FP8X4),
-                lhsT_scale=hs[:, tcols],
+                lhsT=hc[:, k, tcols].bitcast(FP8X4),
+                lhsT_scale=hs[:, k, tcols],
                 rhs=w2c[:].bitcast(FP8X4),
                 rhs_scale=w2s[:],
                 start=True,
                 stop=True,
             )
+
+        def addb(k, t):
+            i = 2 * k + t
             nc.vector.tensor_tensor(
-                out=o_sb[:, i].rearrange("p g c -> p (g c)"),
-                in0=pf[:],
+                out=o_sb[:, SHIFT + O * i : SHIFT + O * (i + 1)],
+                in0=banks[("l2", k, t)][:],
                 in1=b2bc[:].rearrange("p g c -> p (g c)"),
                 op=ALU.add,
             )
-            nc.scalar.activation(out=o_sb[:, i, :, 0:7], in_=o_sb[:, i, :, 0:7], func=ACT.Tanh, scale=0.5)
-            nc.scalar.activation(out=sq[:, i], in_=o_sb[:, i, :, 7:11], func=ACT.Square)
-            nc.vector.tensor_reduce(out=ss[:, i, :], in_=sq[:, i], axis=AX.X, op=ALU.add)
+
+        def sqr(k):
+            nc.scalar.activation(out=sq[k][:], in_=oc(k)[:, :, 7:11], func=ACT.Square)
+
+        def red(k):
+            nc.vector.tensor_reduce(out=ss[:, 64 * k : 64 * k + 64], in_=sq[k][:], axis=AX.X, op=ALU.add)
+
+        def th(k):
+            nc.scalar.activation(out=tht[k][:], in_=oc(k)[:, :, 0:7], func=ACT.Tanh, scale=0.5)
+
+        def clip(k):
             nc.vector.tensor_scalar(
-                out=o_sb[:, i, :, 11:16], in0=o_sb[:, i, :, 11:16],
-                scalar1=0.0, scalar2=1.0, op0=ALU.max, op1=ALU.min,
+                out=oc(k)[:, :, 11:16], in0=oc(k)[:, :, 11:16], scalar1=0.0, scalar2=1.0, op0=ALU.max, op1=ALU.min
             )
+
+        def opc(k):
             nc.vector.scalar_tensor_tensor(
-                out=o_sb[:, i, :, 0:3], in0=o_sb[:, i, :, 0:3], scalar=0.1,
-                in1=a3[:, i, :].unsqueeze(1).to_broadcast([P, NG, 3]),
+                out=oc(k)[:, :, 0:3], in0=tht[k][:, :, 0:3], scalar=0.1,
+                in1=a3x[:, 2 * k : 2 * k + 2].rearrange("p i g c -> p (i g) c"),
                 op0=ALU.mult, op1=ALU.add,
             )
+
+        def opd(k):
             nc.vector.scalar_tensor_tensor(
-                out=o_sb[:, i, :, 3:7], in0=o_sb[:, i, :, 3:7], scalar=1.0,
-                in1=s4[:].unsqueeze(1).to_broadcast([P, NG, 4]),
+                out=oc(k)[:, :, 3:7], in0=tht[k][:, :, 3:7], scalar=1.0,
+                in1=s4[:].unsqueeze(1).to_broadcast([P, 2 * NG, 4]),
                 op0=ALU.add, op1=ALU.mult,
             )
-        nc.vector.tensor_scalar_max(out=ss[:], in0=ss[:], scalar1=1e-24)
-        nc.scalar.activation(out=nrm[:], in_=ss[:], func=ACT.Sqrt)
-        nc.vector.reciprocal(out=rn[:], in_=nrm[:])
-        for i in range(NT):
+
+        def clamp(b):
+            nc.vector.tensor_scalar_max(out=ss[:, 128 * b : 128 * b + 128], in0=ss[:, 128 * b : 128 * b + 128], scalar1=1e-24)
+
+        def sqrt(b):
+            nc.scalar.activation(out=nrm[:, 128 * b : 128 * b + 128], in_=ss[:, 128 * b : 128 * b + 128], func=ACT.Sqrt)
+
+        def rcp(b):
+            nc.vector.reciprocal(out=rn[:, 128 * b : 128 * b + 128], in_=nrm[:, 128 * b : 128 * b + 128])
+
+        def opj(k):
             nc.vector.tensor_tensor(
-                out=o_sb[:, i, :, 7:11], in0=o_sb[:, i, :, 7:11],
-                in1=rn[:, i, :].unsqueeze(2).to_broadcast([P, NG, 4]),
+                out=oc(k)[:, :, 7:11], in0=oc(k)[:, :, 7:11],
+                in1=rn[:, 64 * k : 64 * k + 64].unsqueeze(2).to_broadcast([P, 2 * NG, 4]),
                 op=ALU.mult,
             )
-            nc.sync.dma_start(out=out_v[:, i, :], in_=o_sb[:, i].rearrange("p g c -> p (g c)"))
+
+        def st(k):
+            nc.sync.dma_start(
+                out=out_v[:, 2 * k : 2 * k + 2, :],
+                in_=o_sb[:, SHIFT + 2 * O * k : SHIFT + 2 * O * (k + 1)].rearrange("p (i f) -> p i f", i=2),
+            )
+
+        fns = {
+            "rgW1v": rgW1v, "rgW1s": rgW1s, "qW1": qW1, "rgW2": rgW2, "qW2": qW2, "tr": tr, "cp": cp, "ql": ql,
+            "l1": l1, "si": si, "rg": rg, "qh": qh, "l2": l2, "A": addb, "sq": sqr, "red": red, "th": th,
+            "clip": clip, "C": opc, "D": opd, "clamp": clamp, "sqrt": sqrt, "rcp": rcp, "J": opj, "st": st, "b2c": b2c,
+        }
+        for item in ORDER:
+            fns[item[0]](*item[1:])

@@ -6,6 +6,7 @@ from concourse.masks import make_identity
 FP8X4 = mybir.dt.float8_e4m3fn_x4
 BF16 = mybir.dt.bfloat16
 F32 = mybir.dt.float32
+I32 = mybir.dt.int32
 U32 = mybir.dt.uint32
 U8 = mybir.dt.uint8
 ACT = mybir.ActivationFunctionType
@@ -23,11 +24,10 @@ NCH = 4
 CT = 256
 SHIFT = 1
 VCOLS = 384
-CP_ON_VECTOR = []
 
 FLOPS = 2 * TOK * D * O + 2 * TOK * O * O
 
-ORDER = [["rgW1v",0],["rgW1s",0],["qW1",0],["rgW1s",1],["b2c"],["rgW1v",1],["tr",0,0],["qW1",1],["tr",0,1],["cp",0,0],["tr",1,0],["cp",0,1],["tr",1,1],["cp",1,0],["ql",0],["cp",1,1],["rgW2"],["l1",0,0],["l1",0,1],["l1",0,2],["si",0,0],["ql",1],["l1",0,3],["si",0,1],["tr",2,0],["si",0,2],["qW2"],["tr",2,1],["si",0,3],["cp",2,0],["rg",0],["l1",1,0],["l1",1,1],["cp",2,1],["qh",0],["l1",1,2],["l1",1,3],["si",1,0],["ql",2],["tr",3,0],["si",1,1],["tr",3,1],["si",1,2],["l2",0,0],["si",1,3],["l2",0,1],["cp",3,0],["l1",2,0],["A",0,0],["cp",3,1],["l1",2,1],["rg",1],["l1",2,2],["l1",2,3],["si",2,0],["qh",1],["si",2,1],["A",0,1],["si",2,2],["l2",1,0],["si",2,3],["ql",3],["l2",1,1],["sq",0],["th",0],["red",0],["l1",3,0],["clip",0],["C",0],["l1",3,1],["l1",3,2],["si",3,0],["D",0],["l1",3,3],["si",3,1],["A",1,0],["si",3,2],["A",1,1],["si",3,3],["rg",2],["sq",1],["th",1],["qh",2],["red",1],["l2",2,0],["clamp",0],["clip",1],["l2",2,1],["C",1],["D",1],["rg",3],["sqrt",0],["qh",3],["A",2,0],["A",2,1],["l2",3,0],["rcp",0],["th",2],["l2",3,1],["J",0],["J",1],["st",0],["sq",2],["clip",2],["A",3,0],["A",3,1],["st",1],["clip",3],["th",3],["C",2],["sq",3],["D",2],["red",2],["C",3],["D",3],["red",3],["clamp",1],["sqrt",1],["rcp",1],["J",2],["J",3],["st",2],["st",3]]
+ORDER = [["rgW1v",0],["rgW1s",0],["rgW1s",1],["b2c"],["qW1",0],["rgW1v",1],["tr",0,0],["qW1",1],["tr",0,1],["cp",0,0],["tr",1,0],["cp",0,1],["ql",0],["tr",1,1],["rgW2"],["l1",0,1],["cp",1,1],["l1",0,0],["cp",1,0],["ql",1],["l1",0,2],["l1",0,3],["si",0,1],["qW2"],["tr",2,1],["si",0,0],["tr",2,0],["si",0,2],["si",0,3],["cp",2,1],["rg",0],["l1",1,1],["l1",1,0],["cp",2,0],["l1",1,2],["qh",0],["l1",1,3],["si",1,1],["ql",2],["l2",0,1],["si",1,2],["l2",0,0],["si",1,0],["A",0,1],["tr",3,1],["si",1,3],["tr",3,0],["rg",1],["cp",3,1],["l1",2,1],["l1",2,0],["cp",3,0],["qh",1],["l1",2,3],["A",0,0],["l1",2,2],["si",2,1],["l2",1,1],["si",2,0],["ql",3],["l2",1,0],["si",2,3],["si",2,2],["A",1,1],["th",0],["l1",3,1],["A",1,0],["l1",3,0],["sq",0],["l1",3,2],["rg",2],["sq",1],["l1",3,3],["si",3,1],["red",0],["si",3,0],["red",1],["si",3,3],["clip",0],["si",3,2],["qh",2],["th",1],["clamp",0],["rg",3],["l2",2,0],["l2",2,1],["D",0],["C",0],["qh",3],["A",2,0],["sqrt",0],["A",2,1],["l2",3,0],["C",1],["l2",3,1],["rcp",0],["A",3,0],["sq",2],["A",3,1],["th",2],["clip",1],["sq",3],["clip",2],["red",2],["th",3],["J",1],["J",0],["red",3],["st",0],["D",2],["D",1],["clamp",1],["C",2],["st",1],["sqrt",1],["rcp",1],["clip",3],["J",2],["J",3],["st",2],["D",3],["C",3],["st",3]]
 
 
 def runs4(dst, src):
@@ -50,37 +50,34 @@ def tile_gaussianrenderer_kernel(tc, xyzs, latents, W1, b1, W2, b2, out):
         keep = ctx.enter_context(tc.tile_pool(name="keep", bufs=1))
         psum = ctx.enter_context(tc.psum_pool(name="psum", bufs=2))
 
+        xyz_sb = keep.tile([P, NT, 3], BF16)
+        nc.sync.dma_start(out=xyz_sb[:], in_=xyz_v)
         warm = keep.tile([P, 1], F32)
         nc.vector.memset(warm[:], 0.0)
         nc.scalar.activation(out=warm[:], in_=warm[:], func=ACT.Silu)
-        zb = keep.tile([P, O], BF16)
+        zb = keep.tile([P, NG, G], BF16)
         nc.vector.memset(zb[:], 0.0)
+        nc.vector.memset(zb[32:33, :, 11:16], 0.5)
         ones = keep.tile([P, P], BF16)
         nc.vector.memset(ones[:], 1.0)
         ident = keep.tile([P, P], F32)
         make_identity(nc, ident[:])
 
-        xyz_sb = keep.tile([P, NT, 3], BF16)
-        nc.scalar.dma_start(out=xyz_sb[:], in_=xyz_v)
         b1_sb = keep.tile([P, 4], BF16)
         with nc.allow_non_contiguous_dma(reason="512 bias values, one to a partition and group"):
             nc.scalar.dma_start(out=b1_sb[:], in_=b1.rearrange("(m p) -> p m", p=P))
-        nc.scalar.dma_start(out=zb[0:1, :], in_=b2.unsqueeze(0))
+        nc.scalar.dma_start(out=zb[0:1].rearrange("o g c -> o (g c)"), in_=b2.unsqueeze(0))
 
         w1r = keep.tile([P, 4, 2 * O], BF16)
         x_sb = keep.tile([P, NT, D], BF16)
         w2r = keep.tile([P, 4, O], BF16)
-
-        def load(what, j):
-            if what == "W1":
-                nc.sync.dma_start(out=w1r[:, 2 * j : 2 * j + 2, :], in_=w1_v[:, 2 * j : 2 * j + 2, :])
-            elif what == "L":
-                nc.sync.dma_start(out=x_sb[:, 2 * j : 2 * j + 2, :], in_=lat_v[:, 2 * j : 2 * j + 2, :])
-            else:
-                nc.sync.dma_start(out=w2r[:], in_=w2_v)
-
-        for what, j in (("W1", 0), ("W1", 1), ("L", 0), ("L", 1), ("W2", 0), ("L", 2), ("L", 3)):
-            load(what, j)
+        for j in range(2):
+            nc.sync.dma_start(out=w1r[:, 2 * j : 2 * j + 2, :], in_=w1_v[:, 2 * j : 2 * j + 2, :])
+        for j in range(2):
+            nc.sync.dma_start(out=x_sb[:, 2 * j : 2 * j + 2, :], in_=lat_v[:, 2 * j : 2 * j + 2, :])
+        nc.sync.dma_start(out=w2r[:], in_=w2_v)
+        for j in range(2, 4):
+            nc.sync.dma_start(out=x_sb[:, 2 * j : 2 * j + 2, :], in_=lat_v[:, 2 * j : 2 * j + 2, :])
 
         s4 = keep.tile([P, 4], F32)
         nc.gpsimd.memset(s4[:], 1.0)
@@ -92,16 +89,13 @@ def tile_gaussianrenderer_kernel(tc, xyzs, latents, W1, b1, W2, b2, out):
             scalar1=1.0, scalar2=0.1, op0=ALU.mult, op1=ALU.add,
         )
         b1f = keep.tile([P, 4], F32)
-        nc.gpsimd.tensor_scalar(out=b1f[:], in0=b1_sb[:], scalar1=1.0, scalar2=0.0, op0=ALU.mult, op1=ALU.add)
         pb = psum.tile([P, O], F32, tag="l2", name="pb")
-        nc.tensor.matmul(out=pb[:], lhsT=ones[:], rhs=zb[:], start=True, stop=True)
-        b2bc = keep.tile([P, NG, G], F32)
+        nc.tensor.matmul(out=pb[:], lhsT=ones[:], rhs=zb[:].rearrange("p g c -> p (g c)"), start=True, stop=True)
+        b2bc = keep.tile([P, O], F32)
 
         def b2c():
-            nc.scalar.copy(out=b2bc[:].rearrange("p g c -> p (g c)"), in_=pb[:])
-            nc.gpsimd.tensor_scalar(
-                out=b2bc[:, :, 11:16], in0=b2bc[:, :, 11:16], scalar1=1.0, scalar2=0.5, op0=ALU.mult, op1=ALU.add
-            )
+            nc.scalar.copy(out=b1f[:], in_=b1_sb[:])
+            nc.scalar.copy(out=b2bc[:], in_=pb[:])
 
         w1g = [keep.tile([P, O, 4], BF16, align_bytes=64, name="w1g%d" % g) for g in range(2)]
         w1c = keep.tile([P, 2, O], U32, align_bytes=64)
@@ -165,16 +159,13 @@ def tile_gaussianrenderer_kernel(tc, xyzs, latents, W1, b1, W2, b2, out):
         def cp(k, g):
             xt_v = banks[("xt", k, g)][:].rearrange("p (u t) -> p t u", u=2)
             dst = lg[k][:].bitcast(F32).rearrange("p (g t u) -> p g t u", g=2, u=2)[:, g]
-            if "%d_%d" % (k, g) in CP_ON_VECTOR:
-                nc.vector.tensor_copy(out=dst, in_=xt_v)
-            else:
-                nc.scalar.copy(out=dst, in_=xt_v)
+            nc.scalar.copy(out=dst, in_=xt_v)
 
         def ql(k):
             nc.vector.quantize_mx(out=lc[:, k, :].bitcast(FP8X4), scales=ls[:, k, :], in_=lg[k][:])
 
         def l1(k, m):
-            if m % 2 == 0:
+            if ("l1", k, m // 2) not in banks:
                 banks[("l1", k, m // 2)] = psum.tile([P, 512], F32, tag="l1", bufs=2, name="l1_%d%d" % (k, m // 2))
             ps = banks[("l1", k, m // 2)][:, (m % 2) * CT : (m % 2) * CT + CT]
             mc = slice(m * P, m * P + P)
@@ -220,10 +211,7 @@ def tile_gaussianrenderer_kernel(tc, xyzs, latents, W1, b1, W2, b2, out):
         def addb(k, t):
             i = 2 * k + t
             nc.vector.tensor_tensor(
-                out=o_sb[:, SHIFT + O * i : SHIFT + O * (i + 1)],
-                in0=banks[("l2", k, t)][:],
-                in1=b2bc[:].rearrange("p g c -> p (g c)"),
-                op=ALU.add,
+                out=o_sb[:, SHIFT + O * i : SHIFT + O * (i + 1)], in0=banks[("l2", k, t)][:], in1=b2bc[:], op=ALU.add
             )
 
         def sqr(k):

@@ -27,7 +27,7 @@ VCOLS = 384
 
 FLOPS = 2 * TOK * D * O + 2 * TOK * O * O
 
-ORDER = [["rgW1v",0],["rgW1s",0],["rgW1s",1],["b2c"],["qW1",0],["rgW1v",1],["tr",0,0],["qW1",1],["tr",0,1],["cp",0,0],["tr",1,0],["cp",0,1],["ql",0],["tr",1,1],["rgW2"],["l1",0,1],["cp",1,1],["l1",0,0],["cp",1,0],["ql",1],["l1",0,2],["l1",0,3],["si",0,1],["qW2"],["tr",2,1],["si",0,0],["tr",2,0],["si",0,2],["si",0,3],["cp",2,1],["rg",0],["l1",1,1],["l1",1,0],["cp",2,0],["l1",1,2],["qh",0],["l1",1,3],["si",1,1],["ql",2],["l2",0,1],["si",1,2],["l2",0,0],["si",1,0],["A",0,1],["tr",3,1],["si",1,3],["tr",3,0],["rg",1],["cp",3,1],["l1",2,1],["l1",2,0],["cp",3,0],["qh",1],["l1",2,3],["A",0,0],["l1",2,2],["si",2,1],["l2",1,1],["si",2,0],["ql",3],["l2",1,0],["si",2,3],["si",2,2],["A",1,1],["th",0],["l1",3,1],["A",1,0],["l1",3,0],["sq",0],["l1",3,2],["rg",2],["sq",1],["l1",3,3],["si",3,1],["red",0],["si",3,0],["red",1],["si",3,3],["clip",0],["si",3,2],["qh",2],["th",1],["clamp",0],["rg",3],["l2",2,0],["l2",2,1],["D",0],["C",0],["qh",3],["A",2,0],["sqrt",0],["A",2,1],["l2",3,0],["C",1],["l2",3,1],["rcp",0],["A",3,0],["sq",2],["A",3,1],["th",2],["clip",1],["sq",3],["clip",2],["red",2],["th",3],["J",1],["J",0],["red",3],["st",0],["D",2],["D",1],["clamp",1],["C",2],["st",1],["sqrt",1],["rcp",1],["clip",3],["J",2],["J",3],["st",2],["D",3],["C",3],["st",3]]
+ORDER = [["rgW1v",0],["rgW1s",0],["rgW1s",1],["b2c"],["qW1",0],["rgW1v",1],["tr",0,0],["qW1",1],["tr",0,1],["cp",0,0],["tr",1,0],["cp",0,1],["ql",0],["tr",1,1],["rgW2"],["l1",0,1],["cp",1,1],["l1",0,0],["cp",1,0],["ql",1],["l1",0,2],["l1",0,3],["si",0,1],["qW2"],["tr",2,1],["si",0,0],["tr",2,0],["si",0,2],["si",0,3],["cp",2,1],["rg",0],["l1",1,1],["l1",1,0],["cp",2,0],["l1",1,2],["qh",0],["l1",1,3],["si",1,1],["ql",2],["l2",0,1],["si",1,2],["l2",0,0],["si",1,0],["A",0,1],["tr",3,1],["si",1,3],["tr",3,0],["rg",1],["cp",3,1],["l1",2,1],["l1",2,0],["cp",3,0],["qh",1],["l1",2,3],["A",0,0],["l1",2,2],["si",2,1],["l2",1,1],["si",2,0],["ql",3],["l2",1,0],["si",2,3],["si",2,2],["A",1,1],["th",0],["l1",3,1],["A",1,0],["l1",3,0],["sq",0],["l1",3,2],["rg",2],["sq",1],["l1",3,3],["si",3,1],["red",0],["si",3,0],["red",1],["si",3,3],["clip",0],["si",3,2],["qh",2],["th",1],["clamp",0],["rg",3],["l2",2,0],["l2",2,1],["D",0],["C",0],["qh",3],["A",2,0],["sqrt",0],["A",2,1],["l2",3,0],["C",1],["l2",3,1],["A",3,0],["sq",2],["A",3,1],["th",2],["clip",1],["sq",3],["clip",2],["red",2],["th",3],["J",1],["J",0],["red",3],["st",0],["D",2],["D",1],["clamp",1],["C",2],["st",1],["sqrt",1],["clip",3],["J",2],["J",3],["st",2],["D",3],["C",3],["st",3]]
 
 
 def runs4(dst, src):
@@ -114,7 +114,6 @@ def tile_gaussianrenderer_kernel(tc, xyzs, latents, W1, b1, W2, b2, out):
         sq = [keep.tile([P, 2 * NG, 4], F32, name="sq%d" % k) for k in range(NCH)]
         tht = [keep.tile([P, 2 * NG, 7], F32, name="tht%d" % k) for k in range(NCH)]
         ss = keep.tile([P, NT * NG], F32)
-        nrm = keep.tile([P, NT * NG], F32)
         rn = keep.tile([P, NT * NG], F32)
         banks = {}
 
@@ -246,10 +245,8 @@ def tile_gaussianrenderer_kernel(tc, xyzs, latents, W1, b1, W2, b2, out):
             nc.vector.tensor_scalar_max(out=ss[:, 128 * b : 128 * b + 128], in0=ss[:, 128 * b : 128 * b + 128], scalar1=1e-24)
 
         def sqrt(b):
-            nc.scalar.activation(out=nrm[:, 128 * b : 128 * b + 128], in_=ss[:, 128 * b : 128 * b + 128], func=ACT.Sqrt)
+            nc.scalar.activation(out=rn[:, 128 * b : 128 * b + 128], in_=ss[:, 128 * b : 128 * b + 128], func=ACT.Abs_reciprocal_sqrt)
 
-        def rcp(b):
-            nc.vector.reciprocal(out=rn[:, 128 * b : 128 * b + 128], in_=nrm[:, 128 * b : 128 * b + 128])
 
         def opj(k):
             nc.vector.tensor_tensor(
@@ -267,7 +264,7 @@ def tile_gaussianrenderer_kernel(tc, xyzs, latents, W1, b1, W2, b2, out):
         fns = {
             "rgW1v": rgW1v, "rgW1s": rgW1s, "qW1": qW1, "rgW2": rgW2, "qW2": qW2, "tr": tr, "cp": cp, "ql": ql,
             "l1": l1, "si": si, "rg": rg, "qh": qh, "l2": l2, "A": addb, "sq": sqr, "red": red, "th": th,
-            "clip": clip, "C": opc, "D": opd, "clamp": clamp, "sqrt": sqrt, "rcp": rcp, "J": opj, "st": st, "b2c": b2c,
+            "clip": clip, "C": opc, "D": opd, "clamp": clamp, "sqrt": sqrt, "J": opj, "st": st, "b2c": b2c,
         }
         for item in ORDER:
             fns[item[0]](*item[1:])

@@ -23,11 +23,12 @@ NG = 32
 NCH = 4
 CT = 256
 SHIFT = 1
+BATCH = [[0,192],[192,256]]
 VCOLS = 384
 
 FLOPS = 2 * TOK * D * O + 2 * TOK * O * O
 
-ORDER = [["rgW1v",0],["rgW1s",0],["rgW1s",1],["b2c"],["qW1",0],["rgW1v",1],["tr",0,0],["qW1",1],["tr",0,1],["cp",0,0],["tr",1,0],["cp",0,1],["ql",0],["tr",1,1],["rgW2"],["l1",0,1],["cp",1,1],["l1",0,0],["cp",1,0],["ql",1],["l1",0,2],["l1",0,3],["si",0,1],["qW2"],["tr",2,1],["si",0,0],["tr",2,0],["si",0,2],["si",0,3],["cp",2,1],["rg",0],["l1",1,1],["l1",1,0],["cp",2,0],["l1",1,2],["qh",0],["l1",1,3],["si",1,1],["ql",2],["l2",0,1],["si",1,2],["l2",0,0],["si",1,0],["A",0,1],["tr",3,1],["si",1,3],["tr",3,0],["rg",1],["cp",3,1],["l1",2,1],["l1",2,0],["cp",3,0],["qh",1],["l1",2,3],["A",0,0],["l1",2,2],["si",2,1],["l2",1,1],["si",2,0],["ql",3],["l2",1,0],["si",2,3],["si",2,2],["A",1,1],["th",0],["l1",3,1],["A",1,0],["l1",3,0],["sq",0],["l1",3,2],["rg",2],["sq",1],["l1",3,3],["si",3,1],["red",0],["si",3,0],["red",1],["si",3,3],["clip",0],["si",3,2],["qh",2],["th",1],["clamp",0],["rg",3],["l2",2,0],["l2",2,1],["D",0],["C",0],["qh",3],["A",2,0],["sqrt",0],["A",2,1],["l2",3,0],["C",1],["l2",3,1],["A",3,0],["sq",2],["A",3,1],["th",2],["clip",1],["sq",3],["clip",2],["red",2],["th",3],["J",1],["J",0],["red",3],["st",0],["D",2],["D",1],["clamp",1],["C",2],["st",1],["sqrt",1],["clip",3],["J",2],["J",3],["st",2],["D",3],["C",3],["st",3]]
+ORDER = [["dm"],["dm"],["dm"],["dm"],["dm"],["dm"],["dm"],["dm"],["dm"],["rgW1v",0],["rgW1s",0],["tr",0,0],["qW1",0],["dm"],["cp",0,0],["dm"],["rgW1v",1],["dm"],["rgW1s",1],["tr",0,1],["cp",0,1],["tr",1,0],["qW1",1],["tr",1,1],["cp",1,0],["ql",0],["pb"],["cp",1,1],["rgW2"],["l1",0,1],["b1f"],["l1",0,0],["l1",0,3],["l1",0,2],["ql",1],["si",0,0],["tr",2,0],["si",0,1],["qW2"],["si",0,3],["tr",2,1],["si",0,2],["cp",2,0],["rg",0],["l1",1,0],["l1",1,3],["cp",2,1],["l1",1,1],["qh",0],["l1",1,2],["b2c"],["ql",2],["l2",0,1],["si",1,1],["l2",0,0],["tr",3,0],["A",0,1],["si",1,2],["si",1,0],["tr",3,1],["A",0,0],["si",1,3],["cp",3,0],["l1",2,1],["rg",1],["l1",2,0],["cp",3,1],["l1",2,3],["qh",1],["l1",2,2],["si",2,1],["ql",3],["si",2,2],["l2",1,0],["clip",0],["l2",1,1],["si",2,0],["dm"],["A",1,0],["si",2,3],["th",0],["l1",3,0],["rg",2],["l1",3,1],["sq",0],["l1",3,2],["C",0],["l1",3,3],["si",3,1],["qh",2],["si",3,0],["A",1,1],["si",3,3],["si",3,2],["red",0],["l2",2,1],["th",1],["rg",3],["l2",2,0],["sq",1],["A",2,1],["A",2,0],["qh",3],["sq",2],["C",1],["th",2],["l2",3,1],["red",2],["l2",3,0],["D",1],["A",3,1],["A",3,0],["red",1],["sq",3],["D",0],["sqrt",0],["red",3],["J",0],["sqrt",1],["clip",1],["st",0],["J",1],["D",2],["C",2],["st",1],["J",2],["clip",3],["th",3],["clip",2],["J",3],["st",2],["C",3],["D",3],["st",3]]
 
 
 def runs4(dst, src):
@@ -52,32 +53,36 @@ def tile_gaussianrenderer_kernel(tc, xyzs, latents, W1, b1, W2, b2, out):
 
         xyz_sb = keep.tile([P, NT, 3], BF16)
         nc.sync.dma_start(out=xyz_sb[:], in_=xyz_v)
-        warm = keep.tile([P, 1], F32)
-        nc.vector.memset(warm[:], 0.0)
-        nc.scalar.activation(out=warm[:], in_=warm[:], func=ACT.Silu)
-        zb = keep.tile([P, NG, G], BF16)
-        nc.vector.memset(zb[:], 0.0)
-        nc.vector.memset(zb[32:33, :, 11:16], 0.5)
-        ones = keep.tile([P, P], BF16)
-        nc.vector.memset(ones[:], 1.0)
-        ident = keep.tile([P, P], F32)
-        make_identity(nc, ident[:])
-
         b1_sb = keep.tile([P, 4], BF16)
         with nc.allow_non_contiguous_dma(reason="512 bias values, one to a partition and group"):
             nc.scalar.dma_start(out=b1_sb[:], in_=b1.rearrange("(m p) -> p m", p=P))
+        zb = keep.tile([P, NG, G], BF16)
+        nc.vector.memset(zb[:], 0.0)
+        nc.vector.memset(zb[32:33, :, 11:16], 0.5)
         nc.scalar.dma_start(out=zb[0:1].rearrange("o g c -> o (g c)"), in_=b2.unsqueeze(0))
+        warm = keep.tile([P, 1], F32)
+        nc.vector.memset(warm[:], 0.0)
+        nc.scalar.activation(out=warm[:], in_=warm[:], func=ACT.Silu)
+        ones = keep.tile([P, P], BF16)
+        dzer = keep.tile([P, 4 * O], BF16, align_bytes=64)
+        nc.vector.memset(dzer[:], 0.0)
+        dcod = keep.tile([P, O], U32, align_bytes=64)
+        dsca = keep.tile([P, O], U8, align_bytes=64)
+        nc.vector.memset(ones[:], 1.0)
+        nc.vector.quantize_mx(out=dcod[:].bitcast(FP8X4), scales=dsca[:], in_=dzer[:])
+        ident = keep.tile([P, P], F32)
+        make_identity(nc, ident[:])
 
         w1r = keep.tile([P, 4, 2 * O], BF16)
         x_sb = keep.tile([P, NT, D], BF16)
         w2r = keep.tile([P, 4, O], BF16)
-        for j in range(2):
-            nc.sync.dma_start(out=w1r[:, 2 * j : 2 * j + 2, :], in_=w1_v[:, 2 * j : 2 * j + 2, :])
-        for j in range(2):
-            nc.sync.dma_start(out=x_sb[:, 2 * j : 2 * j + 2, :], in_=lat_v[:, 2 * j : 2 * j + 2, :])
-        nc.sync.dma_start(out=w2r[:], in_=w2_v)
-        for j in range(2, 4):
-            nc.sync.dma_start(out=x_sb[:, 2 * j : 2 * j + 2, :], in_=lat_v[:, 2 * j : 2 * j + 2, :])
+        for what, j in (("W1", 0), ("L", 0), ("W1", 1), ("L", 1), ("W2", 0), ("L", 2), ("L", 3)):
+            if what == "W1":
+                nc.sync.dma_start(out=w1r[:, 2 * j : 2 * j + 2, :], in_=w1_v[:, 2 * j : 2 * j + 2, :])
+            elif what == "L":
+                nc.sync.dma_start(out=x_sb[:, 2 * j : 2 * j + 2, :], in_=lat_v[:, 2 * j : 2 * j + 2, :])
+            else:
+                nc.sync.dma_start(out=w2r[:], in_=w2_v)
 
         s4 = keep.tile([P, 4], F32)
         nc.gpsimd.memset(s4[:], 1.0)
@@ -89,13 +94,20 @@ def tile_gaussianrenderer_kernel(tc, xyzs, latents, W1, b1, W2, b2, out):
             scalar1=1.0, scalar2=0.1, op0=ALU.mult, op1=ALU.add,
         )
         b1f = keep.tile([P, 4], F32)
-        pb = psum.tile([P, O], F32, tag="l2", name="pb")
-        nc.tensor.matmul(out=pb[:], lhsT=ones[:], rhs=zb[:].rearrange("p g c -> p (g c)"), start=True, stop=True)
         b2bc = keep.tile([P, O], F32)
+        banks = {}
+
+        def pbm():
+            banks["pb"] = psum.tile([P, O], F32, tag="l2", bufs=2, name="pb")
+            nc.tensor.matmul(
+                out=banks["pb"][:], lhsT=ones[:], rhs=zb[:].rearrange("p g c -> p (g c)"), start=True, stop=True
+            )
+
+        def b1c():
+            nc.scalar.copy(out=b1f[:], in_=b1_sb[:])
 
         def b2c():
-            nc.scalar.copy(out=b1f[:], in_=b1_sb[:])
-            nc.scalar.copy(out=b2bc[:], in_=pb[:])
+            nc.scalar.copy(out=b2bc[:], in_=banks["pb"][:])
 
         w1g = [keep.tile([P, O, 4], BF16, align_bytes=64, name="w1g%d" % g) for g in range(2)]
         w1c = keep.tile([P, 2, O], U32, align_bytes=64)
@@ -115,7 +127,6 @@ def tile_gaussianrenderer_kernel(tc, xyzs, latents, W1, b1, W2, b2, out):
         tht = [keep.tile([P, 2 * NG, 7], F32, name="tht%d" % k) for k in range(NCH)]
         ss = keep.tile([P, NT * NG], F32)
         rn = keep.tile([P, NT * NG], F32)
-        banks = {}
 
         def oc(k):
             return o_sb[:, SHIFT + 2 * O * k : SHIFT + 2 * O * (k + 1)].rearrange("p (q c) -> p q c", c=G)
@@ -144,7 +155,7 @@ def tile_gaussianrenderer_kernel(tc, xyzs, latents, W1, b1, W2, b2, out):
             nc.vector.quantize_mx(out=w2c[:].bitcast(FP8X4), scales=w2s[:], in_=w2g[:].rearrange("p c t -> p (c t)"))
 
         def tr(k, g):
-            xt = psum.tile([P, 512], F32, tag="xt", bufs=4, name="xt%d%d" % (k, g))
+            xt = psum.tile([P, 512], F32, tag="xt", bufs=3, name="xt%d%d" % (k, g))
             banks[("xt", k, g)] = xt
             xt_v = xt[:].rearrange("p (u t) -> p u t", u=2)
             for il in range(2):
@@ -207,6 +218,19 @@ def tile_gaussianrenderer_kernel(tc, xyzs, latents, W1, b1, W2, b2, out):
                 stop=True,
             )
 
+        def dm():
+            if "dm" not in banks:
+                banks["dm"] = psum.tile([P, 512], F32, tag="dm", bufs=1, name="dmb")
+            nc.tensor.matmul_mx(
+                out=banks["dm"][:],
+                lhsT=dcod[:, 0:P].bitcast(FP8X4),
+                lhsT_scale=dsca[:, 0:P],
+                rhs=dcod[:].bitcast(FP8X4),
+                rhs_scale=dsca[:],
+                start=True,
+                stop=True,
+            )
+
         def addb(k, t):
             i = 2 * k + t
             nc.vector.tensor_tensor(
@@ -241,18 +265,15 @@ def tile_gaussianrenderer_kernel(tc, xyzs, latents, W1, b1, W2, b2, out):
                 op0=ALU.add, op1=ALU.mult,
             )
 
-        def clamp(b):
-            nc.vector.tensor_scalar_max(out=ss[:, 128 * b : 128 * b + 128], in0=ss[:, 128 * b : 128 * b + 128], scalar1=1e-24)
-
         def sqrt(b):
-            nc.scalar.activation(out=rn[:, 128 * b : 128 * b + 128], in_=ss[:, 128 * b : 128 * b + 128], func=ACT.Abs_reciprocal_sqrt)
-
+            lo, hi = BATCH[b]
+            nc.scalar.activation(out=rn[:, lo:hi], in_=ss[:, lo:hi], func=ACT.Abs_reciprocal_sqrt)
 
         def opj(k):
-            nc.vector.tensor_tensor(
-                out=oc(k)[:, :, 7:11], in0=oc(k)[:, :, 7:11],
-                in1=rn[:, 64 * k : 64 * k + 64].unsqueeze(2).to_broadcast([P, 2 * NG, 4]),
-                op=ALU.mult,
+            nc.vector.scalar_tensor_tensor(
+                out=oc(k)[:, :, 7:11],
+                in0=rn[:, 64 * k : 64 * k + 64].unsqueeze(2).to_broadcast([P, 2 * NG, 4]),
+                scalar=1e12, in1=oc(k)[:, :, 7:11], op0=ALU.min, op1=ALU.mult,
             )
 
         def st(k):
@@ -264,7 +285,7 @@ def tile_gaussianrenderer_kernel(tc, xyzs, latents, W1, b1, W2, b2, out):
         fns = {
             "rgW1v": rgW1v, "rgW1s": rgW1s, "qW1": qW1, "rgW2": rgW2, "qW2": qW2, "tr": tr, "cp": cp, "ql": ql,
             "l1": l1, "si": si, "rg": rg, "qh": qh, "l2": l2, "A": addb, "sq": sqr, "red": red, "th": th,
-            "clip": clip, "C": opc, "D": opd, "clamp": clamp, "sqrt": sqrt, "J": opj, "st": st, "b2c": b2c,
+            "clip": clip, "C": opc, "D": opd, "sqrt": sqrt, "J": opj, "st": st, "b2c": b2c, "b1f": b1c, "pb": pbm, "dm": dm,
         }
         for item in ORDER:
             fns[item[0]](*item[1:])

@@ -6,32 +6,29 @@ from concourse.masks import make_identity
 FP8X4 = mybir.dt.float8_e4m3fn_x4
 BF16 = mybir.dt.bfloat16
 F32 = mybir.dt.float32
-I32 = mybir.dt.int32
 U32 = mybir.dt.uint32
 U8 = mybir.dt.uint8
 ACT = mybir.ActivationFunctionType
 ALU = mybir.AluOpType
-AX = mybir.AxisListType
 
 P = 128
-TOK = 1024
-D = 1024
-O = 512
-NT = 8
-G = 16
-NG = 32
-NCH = 4
-CT = 256
-SHIFT = 1
-BATCH = [[0,192],[192,256]]
-VCOLS = 384
+TOKENS = 1024
+K1 = 1024
+WIDTH = 512
+TILES = TOKENS // P
+GAUSS = 32
+CH = 16
+CHUNKS = 4
+CHUNK = TOKENS // CHUNKS
+ROWS = 2 * GAUSS
+GROUPS = WIDTH // P
+W1_VECTOR_COLS = 384
+LEAD = 1
 
-FLOPS = 2 * TOK * D * O + 2 * TOK * O * O
-
-ORDER = [["dm"],["dm"],["dm"],["dm"],["dm"],["dm"],["dm"],["dm"],["dm"],["rgW1v",0],["rgW1s",0],["tr",0,0],["qW1",0],["dm"],["cp",0,0],["dm"],["rgW1v",1],["dm"],["rgW1s",1],["tr",0,1],["cp",0,1],["tr",1,0],["qW1",1],["tr",1,1],["cp",1,0],["ql",0],["pb"],["cp",1,1],["rgW2"],["l1",0,1],["b1f"],["l1",0,0],["l1",0,3],["l1",0,2],["ql",1],["si",0,0],["tr",2,0],["si",0,1],["qW2"],["si",0,3],["tr",2,1],["si",0,2],["cp",2,0],["rg",0],["l1",1,0],["l1",1,3],["cp",2,1],["l1",1,1],["qh",0],["l1",1,2],["b2c"],["ql",2],["l2",0,1],["si",1,1],["l2",0,0],["tr",3,0],["A",0,1],["si",1,2],["si",1,0],["tr",3,1],["A",0,0],["si",1,3],["cp",3,0],["l1",2,1],["rg",1],["l1",2,0],["cp",3,1],["l1",2,3],["qh",1],["l1",2,2],["si",2,1],["ql",3],["si",2,2],["l2",1,0],["clip",0],["l2",1,1],["si",2,0],["dm"],["A",1,0],["si",2,3],["th",0],["l1",3,0],["rg",2],["l1",3,1],["sq",0],["l1",3,2],["C",0],["l1",3,3],["si",3,1],["qh",2],["si",3,0],["A",1,1],["si",3,3],["si",3,2],["red",0],["l2",2,1],["th",1],["rg",3],["l2",2,0],["sq",1],["A",2,1],["A",2,0],["qh",3],["sq",2],["C",1],["th",2],["l2",3,1],["red",2],["l2",3,0],["D",1],["A",3,1],["A",3,0],["red",1],["sq",3],["D",0],["sqrt",0],["red",3],["J",0],["sqrt",1],["clip",1],["st",0],["J",1],["D",2],["C",2],["st",1],["J",2],["clip",3],["th",3],["clip",2],["J",3],["st",2],["C",3],["D",3],["st",3]]
+FLOPS = 2 * TOKENS * K1 * WIDTH + 2 * TOKENS * WIDTH * WIDTH
 
 
-def runs4(dst, src):
+def side_by_side(dst, src):
     return (
         dst.rearrange("p (c i) t -> p c t i", i=4),
         src.rearrange("p t (c i) -> p c t i", i=4),
@@ -40,9 +37,9 @@ def runs4(dst, src):
 
 def tile_gaussianrenderer_kernel(tc, xyzs, latents, W1, b1, W2, b2, out):
     nc = tc.nc
-    lat_v = latents.rearrange("b n d -> (b n) d").rearrange("(p i) d -> p i d", i=NT)
-    xyz_v = xyzs.rearrange("b n c -> (b n) c").rearrange("(p i) c -> p i c", i=NT)
-    out_v = out.rearrange("b (n g) c -> (b n) (g c)", g=NG).rearrange("(p i) f -> p i f", i=NT)
+    lat_v = latents.rearrange("b n d -> (b n) d").rearrange("(p i) d -> p i d", i=TILES)
+    xyz_v = xyzs.rearrange("b n c -> (b n) c").rearrange("(p i) c -> p i c", i=TILES)
+    out_v = out.rearrange("b (n g) c -> (b n) (g c)", g=GAUSS).rearrange("(p i) f -> p i f", i=TILES)
     w1_v = W1.rearrange("(a q e) c -> q a (e c)", a=4, e=2)
     w2_v = W2.rearrange("(t p) n -> p t n", p=P)
 
@@ -51,241 +48,274 @@ def tile_gaussianrenderer_kernel(tc, xyzs, latents, W1, b1, W2, b2, out):
         keep = ctx.enter_context(tc.tile_pool(name="keep", bufs=1))
         psum = ctx.enter_context(tc.psum_pool(name="psum", bufs=2))
 
-        xyz_sb = keep.tile([P, NT, 3], BF16)
+        xyz_sb = keep.tile([P, TILES, 3], BF16)
+        b1_sb = keep.tile([P, GROUPS], BF16)
+        bias_rows = keep.tile([P, GAUSS, CH], BF16)
+        w1_raw = keep.tile([P, 4, 2 * WIDTH], BF16)
+        lat_sb = keep.tile([P, TILES, K1], BF16)
+        w2_raw = keep.tile([P, 4, WIDTH], BF16)
+
         nc.sync.dma_start(out=xyz_sb[:], in_=xyz_v)
-        b1_sb = keep.tile([P, 4], BF16)
-        with nc.allow_non_contiguous_dma(reason="512 bias values, one to a partition and group"):
+        with nc.allow_non_contiguous_dma(reason="b1[128 m + p] goes to partition p, column m"):
             nc.scalar.dma_start(out=b1_sb[:], in_=b1.rearrange("(m p) -> p m", p=P))
-        zb = keep.tile([P, NG, G], BF16)
-        nc.vector.memset(zb[:], 0.0)
-        nc.vector.memset(zb[32:33, :, 11:16], 0.5)
-        nc.scalar.dma_start(out=zb[0:1].rearrange("o g c -> o (g c)"), in_=b2.unsqueeze(0))
+        nc.vector.memset(bias_rows[:], 0.0)
+        nc.vector.memset(bias_rows[32:33, :, 11:16], 0.5)
+        nc.scalar.dma_start(out=bias_rows[0:1].rearrange("o g c -> o (g c)"), in_=b2.unsqueeze(0))
+        for g in range(2):
+            nc.sync.dma_start(out=w1_raw[:, 2 * g : 2 * g + 2, :], in_=w1_v[:, 2 * g : 2 * g + 2, :])
+        for k in (0, 1):
+            nc.sync.dma_start(out=lat_sb[:, 2 * k : 2 * k + 2, :], in_=lat_v[:, 2 * k : 2 * k + 2, :])
+        nc.sync.dma_start(out=w2_raw[:], in_=w2_v)
+        for k in (2, 3):
+            nc.sync.dma_start(out=lat_sb[:, 2 * k : 2 * k + 2, :], in_=lat_v[:, 2 * k : 2 * k + 2, :])
+
         warm = keep.tile([P, 1], F32)
         nc.vector.memset(warm[:], 0.0)
         nc.scalar.activation(out=warm[:], in_=warm[:], func=ACT.Silu)
         ones = keep.tile([P, P], BF16)
-        dzer = keep.tile([P, 4 * O], BF16, align_bytes=64)
-        nc.vector.memset(dzer[:], 0.0)
-        dcod = keep.tile([P, O], U32, align_bytes=64)
-        dsca = keep.tile([P, O], U8, align_bytes=64)
         nc.vector.memset(ones[:], 1.0)
-        nc.vector.quantize_mx(out=dcod[:].bitcast(FP8X4), scales=dsca[:], in_=dzer[:])
         ident = keep.tile([P, P], F32)
         make_identity(nc, ident[:])
-
-        w1r = keep.tile([P, 4, 2 * O], BF16)
-        x_sb = keep.tile([P, NT, D], BF16)
-        w2r = keep.tile([P, 4, O], BF16)
-        for what, j in (("W1", 0), ("L", 0), ("W1", 1), ("L", 1), ("W2", 0), ("L", 2), ("L", 3)):
-            if what == "W1":
-                nc.sync.dma_start(out=w1r[:, 2 * j : 2 * j + 2, :], in_=w1_v[:, 2 * j : 2 * j + 2, :])
-            elif what == "L":
-                nc.sync.dma_start(out=x_sb[:, 2 * j : 2 * j + 2, :], in_=lat_v[:, 2 * j : 2 * j + 2, :])
-            else:
-                nc.sync.dma_start(out=w2r[:], in_=w2_v)
-
-        s4 = keep.tile([P, 4], F32)
-        nc.gpsimd.memset(s4[:], 1.0)
-        nc.gpsimd.tensor_scalar(out=s4[:, 0:1], in0=s4[:, 0:1], scalar1=0.5, scalar2=0.0, op0=ALU.mult, op1=ALU.add)
-        nc.gpsimd.tensor_scalar(out=s4[:, 1:4], in0=s4[:, 1:4], scalar1=0.01, scalar2=0.0, op0=ALU.mult, op1=ALU.add)
-        a3x = keep.tile([P, NT, NG, 3], F32)
+        half_scale = keep.tile([P, 4], F32)
+        nc.gpsimd.memset(half_scale[:], 1.0)
+        for cols, factor in ((slice(0, 1), 0.5), (slice(1, 4), 0.01)):
+            nc.gpsimd.tensor_scalar(
+                out=half_scale[:, cols], in0=half_scale[:, cols],
+                scalar1=factor, scalar2=0.0, op0=ALU.mult, op1=ALU.add,
+            )
+        centre = keep.tile([P, TILES, GAUSS, 3], F32)
         nc.gpsimd.tensor_scalar(
-            out=a3x[:], in0=xyz_sb[:].unsqueeze(2).to_broadcast([P, NT, NG, 3]),
+            out=centre[:], in0=xyz_sb[:].unsqueeze(2).to_broadcast([P, TILES, GAUSS, 3]),
             scalar1=1.0, scalar2=0.1, op0=ALU.mult, op1=ALU.add,
         )
-        b1f = keep.tile([P, 4], F32)
-        b2bc = keep.tile([P, O], F32)
+
+        b1_f32 = keep.tile([P, GROUPS], F32)
+        bias_all = keep.tile([P, WIDTH], F32)
+        w1_grouped = [keep.tile([P, WIDTH, 4], BF16, align_bytes=64, name="w1_grouped%d" % g) for g in range(2)]
+        w1_codes = keep.tile([P, 2, WIDTH], U32, align_bytes=64)
+        w1_scales = keep.tile([P, 2, WIDTH], U8, align_bytes=64)
+        w2_grouped = keep.tile([P, WIDTH, 4], BF16, align_bytes=64)
+        w2_codes = keep.tile([P, WIDTH], U32, align_bytes=64)
+        w2_scales = keep.tile([P, WIDTH], U8, align_bytes=64)
+        lat_grouped = [keep.tile([P, 8 * CHUNK], BF16, align_bytes=64, name="lat_grouped%d" % k) for k in range(CHUNKS)]
+        lat_codes = keep.tile([P, CHUNKS, 2 * CHUNK], U32, align_bytes=64)
+        lat_scales = keep.tile([P, CHUNKS, 2 * CHUNK], U8, align_bytes=64)
+        h_planes = [keep.tile([P, GROUPS, CHUNK], BF16, name="h_planes%d" % k) for k in range(CHUNKS)]
+        h_grouped = [keep.tile([P, CHUNK, 4], BF16, align_bytes=64, name="h_grouped%d" % k) for k in range(CHUNKS)]
+        h_codes = keep.tile([P, CHUNKS, CHUNK], U32, align_bytes=64)
+        h_scales = keep.tile([P, CHUNKS, CHUNK], U8, align_bytes=64)
+        out_sb = keep.tile([P, TILES * WIDTH + 4], F32)
+        tanh_sb = [keep.tile([P, ROWS, 7], F32, name="tanh_sb%d" % k) for k in range(CHUNKS)]
+        squares = [keep.tile([P, ROWS, 4], F32, name="squares%d" % k) for k in range(CHUNKS)]
+        norm2 = keep.tile([P, CHUNKS * ROWS], F32)
+        inv_norm = keep.tile([P, CHUNKS * ROWS], F32)
         banks = {}
 
-        def pbm():
-            banks["pb"] = psum.tile([P, O], F32, tag="l2", bufs=2, name="pb")
-            nc.tensor.matmul(
-                out=banks["pb"][:], lhsT=ones[:], rhs=zb[:].rearrange("p g c -> p (g c)"), start=True, stop=True
-            )
+        def channels(k):
+            first = LEAD + 2 * WIDTH * k
+            return out_sb[:, first : first + 2 * WIDTH].rearrange("p (r c) -> p r c", c=CH)
 
-        def b1c():
-            nc.scalar.copy(out=b1f[:], in_=b1_sb[:])
+        def w1_rows(g):
+            return w1_raw[:, 2 * g : 2 * g + 2, :].rearrange("p u (e c) -> p (u e) c", e=2)
 
-        def b2c():
-            nc.scalar.copy(out=b2bc[:], in_=banks["pb"][:])
+        def regroup_w1_vector(g):
+            dst, src = side_by_side(w1_grouped[g][:, 0:W1_VECTOR_COLS, :], w1_rows(g)[:, :, 0:W1_VECTOR_COLS])
+            nc.vector.tensor_copy(out=dst, in_=src)
 
-        w1g = [keep.tile([P, O, 4], BF16, align_bytes=64, name="w1g%d" % g) for g in range(2)]
-        w1c = keep.tile([P, 2, O], U32, align_bytes=64)
-        w1s = keep.tile([P, 2, O], U8, align_bytes=64)
-        w2g = keep.tile([P, O, 4], BF16, align_bytes=64)
-        w2c = keep.tile([P, O], U32, align_bytes=64)
-        w2s = keep.tile([P, O], U8, align_bytes=64)
-        lg = [keep.tile([P, 8 * CT], BF16, align_bytes=64, name="lg%d" % k) for k in range(NCH)]
-        lc = keep.tile([P, NCH, 2 * CT], U32, align_bytes=64)
-        ls = keep.tile([P, NCH, 2 * CT], U8, align_bytes=64)
-        hp = [keep.tile([P, 4, CT], BF16, name="hp%d" % k) for k in range(NCH)]
-        hg = [keep.tile([P, CT, 4], BF16, align_bytes=64, name="hg%d" % k) for k in range(NCH)]
-        hc = keep.tile([P, NCH, CT], U32, align_bytes=64)
-        hs = keep.tile([P, NCH, CT], U8, align_bytes=64)
-        o_sb = keep.tile([P, NT * O + 4], F32)
-        sq = [keep.tile([P, 2 * NG, 4], F32, name="sq%d" % k) for k in range(NCH)]
-        tht = [keep.tile([P, 2 * NG, 7], F32, name="tht%d" % k) for k in range(NCH)]
-        ss = keep.tile([P, NT * NG], F32)
-        rn = keep.tile([P, NT * NG], F32)
+        def regroup_w1_scalar(g):
+            dst, src = side_by_side(w1_grouped[g][:, W1_VECTOR_COLS:, :], w1_rows(g)[:, :, W1_VECTOR_COLS:])
+            nc.scalar.copy(out=dst, in_=src)
 
-        def oc(k):
-            return o_sb[:, SHIFT + 2 * O * k : SHIFT + 2 * O * (k + 1)].rearrange("p (q c) -> p q c", c=G)
-
-        def w1src(g):
-            return w1r[:, 2 * g : 2 * g + 2, :].rearrange("p u (e c) -> p (u e) c", e=2)
-
-        def rgW1v(g):
-            d, s = runs4(w1g[g][:, 0:VCOLS, :], w1src(g)[:, :, 0:VCOLS])
-            nc.vector.tensor_copy(out=d, in_=s)
-
-        def rgW1s(g):
-            d, s = runs4(w1g[g][:, VCOLS:O, :], w1src(g)[:, :, VCOLS:O])
-            nc.scalar.copy(out=d, in_=s)
-
-        def qW1(g):
+        def quantise_w1(g):
             nc.vector.quantize_mx(
-                out=w1c[:, g, :].bitcast(FP8X4), scales=w1s[:, g, :], in_=w1g[g][:].rearrange("p c t -> p (c t)")
+                out=w1_codes[:, g, :].bitcast(FP8X4), scales=w1_scales[:, g, :],
+                in_=w1_grouped[g][:].rearrange("p c t -> p (c t)"),
             )
 
-        def rgW2():
-            d, s = runs4(w2g[:], w2r[:])
-            nc.vector.tensor_copy(out=d, in_=s)
+        def regroup_w2():
+            dst, src = side_by_side(w2_grouped[:], w2_raw[:])
+            nc.vector.tensor_copy(out=dst, in_=src)
 
-        def qW2():
-            nc.vector.quantize_mx(out=w2c[:].bitcast(FP8X4), scales=w2s[:], in_=w2g[:].rearrange("p c t -> p (c t)"))
+        def quantise_w2():
+            nc.vector.quantize_mx(
+                out=w2_codes[:].bitcast(FP8X4), scales=w2_scales[:], in_=w2_grouped[:].rearrange("p c t -> p (c t)")
+            )
 
-        def tr(k, g):
-            xt = psum.tile([P, 512], F32, tag="xt", bufs=3, name="xt%d%d" % (k, g))
-            banks[("xt", k, g)] = xt
-            xt_v = xt[:].rearrange("p (u t) -> p u t", u=2)
-            for il in range(2):
-                x32 = x_sb[:, 2 * k + il, :].bitcast(F32)
-                for u in range(2):
-                    w0 = 256 * g + 128 * u
-                    nc.tensor.transpose(
-                        out=xt_v[:, u, il * P : il * P + P], in_=x32[:, w0 : w0 + P], identity=ident[:]
+        def spread_bias():
+            banks["bias"] = psum.tile([P, WIDTH], F32, tag="f", bufs=2, name="bias_bank")
+            nc.tensor.matmul(
+                out=banks["bias"][:], lhsT=ones[:], rhs=bias_rows[:].rearrange("p g c -> p (g c)"),
+                start=True, stop=True,
+            )
+
+        def transpose_latents(k):
+            for g in range(2):
+                bank = psum.tile([P, 2, CHUNK], F32, tag="latT", bufs=4, name="latT%d%d" % (k, g))
+                banks[("latT", k, g)] = bank
+                for i in range(2):
+                    words = lat_sb[:, 2 * k + i, :].bitcast(F32)
+                    for u in range(2):
+                        first = 256 * g + 128 * u
+                        nc.tensor.transpose(
+                            out=bank[:, u, i * P : (i + 1) * P], in_=words[:, first : first + P], identity=ident[:]
+                        )
+
+        def copy_latents(k):
+            grouped = lat_grouped[k][:].bitcast(F32).rearrange("p (g n u) -> p g n u", g=2, u=2)
+            for g in range(2):
+                nc.scalar.copy(out=grouped[:, g], in_=banks[("latT", k, g)][:].rearrange("p u n -> p n u"))
+
+        def quantise_latents(k):
+            nc.vector.quantize_mx(
+                out=lat_codes[:, k, :].bitcast(FP8X4), scales=lat_scales[:, k, :], in_=lat_grouped[k][:]
+            )
+
+        def layer1(k):
+            for m in range(GROUPS):
+                if m % 2 == 0:
+                    banks[("hT", k, m // 2)] = psum.tile([P, 2, CHUNK], F32, tag="hT", bufs=2, name="hT%d%d" % (k, m // 2))
+                cols = slice(m * P, (m + 1) * P)
+                for g in range(2):
+                    toks = slice(g * CHUNK, (g + 1) * CHUNK)
+                    nc.tensor.matmul_mx(
+                        out=banks[("hT", k, m // 2)][:, m % 2, :],
+                        lhsT=w1_codes[:, g, cols].bitcast(FP8X4),
+                        lhsT_scale=w1_scales[:, g, cols],
+                        rhs=lat_codes[:, k, toks].bitcast(FP8X4),
+                        rhs_scale=lat_scales[:, k, toks],
+                        start=(g == 0),
+                        stop=(g == 1),
                     )
 
-        def cp(k, g):
-            xt_v = banks[("xt", k, g)][:].rearrange("p (u t) -> p t u", u=2)
-            dst = lg[k][:].bitcast(F32).rearrange("p (g t u) -> p g t u", g=2, u=2)[:, g]
-            nc.scalar.copy(out=dst, in_=xt_v)
-
-        def ql(k):
-            nc.vector.quantize_mx(out=lc[:, k, :].bitcast(FP8X4), scales=ls[:, k, :], in_=lg[k][:])
-
-        def l1(k, m):
-            if ("l1", k, m // 2) not in banks:
-                banks[("l1", k, m // 2)] = psum.tile([P, 512], F32, tag="l1", bufs=2, name="l1_%d%d" % (k, m // 2))
-            ps = banks[("l1", k, m // 2)][:, (m % 2) * CT : (m % 2) * CT + CT]
-            mc = slice(m * P, m * P + P)
-            for g in range(2):
-                tcols = slice(g * CT, g * CT + CT)
-                nc.tensor.matmul_mx(
-                    out=ps,
-                    lhsT=w1c[:, g, mc].bitcast(FP8X4),
-                    lhsT_scale=w1s[:, g, mc],
-                    rhs=lc[:, k, tcols].bitcast(FP8X4),
-                    rhs_scale=ls[:, k, tcols],
-                    start=(g == 0),
-                    stop=(g == 1),
+        def silu(k):
+            for m in range(GROUPS):
+                nc.scalar.activation(
+                    out=h_planes[k][:, m, :], in_=banks[("hT", k, m // 2)][:, m % 2, :],
+                    func=ACT.Silu, bias=b1_f32[:, m : m + 1], scale=1.0,
                 )
 
-        def si(k, m):
-            ps = banks[("l1", k, m // 2)][:, (m % 2) * CT : (m % 2) * CT + CT]
-            nc.scalar.activation(out=hp[k][:, m, :], in_=ps, func=ACT.Silu, bias=b1f[:, m : m + 1], scale=1.0)
+        def regroup_h(k):
+            dst, src = side_by_side(h_grouped[k][:], h_planes[k][:])
+            nc.vector.tensor_copy(out=dst, in_=src)
 
-        def rg(k):
-            d, s = runs4(hg[k][:], hp[k][:])
-            nc.vector.tensor_copy(out=d, in_=s)
-
-        def qh(k):
+        def quantise_h(k):
             nc.vector.quantize_mx(
-                out=hc[:, k, :].bitcast(FP8X4), scales=hs[:, k, :], in_=hg[k][:].rearrange("p c t -> p (c t)")
+                out=h_codes[:, k, :].bitcast(FP8X4), scales=h_scales[:, k, :],
+                in_=h_grouped[k][:].rearrange("p n t -> p (n t)"),
             )
 
-        def l2(k, t):
-            pf = psum.tile([P, 512], F32, tag="l2", bufs=2, name="l2_%d%d" % (k, t))
-            banks[("l2", k, t)] = pf
-            tcols = slice(t * P, t * P + P)
-            nc.tensor.matmul_mx(
-                out=pf[:],
-                lhsT=hc[:, k, tcols].bitcast(FP8X4),
-                lhsT_scale=hs[:, k, tcols],
-                rhs=w2c[:].bitcast(FP8X4),
-                rhs_scale=w2s[:],
-                start=True,
-                stop=True,
-            )
+        def layer2(k):
+            for i in range(2):
+                banks[("f", k, i)] = psum.tile([P, WIDTH], F32, tag="f", bufs=2, name="f%d%d" % (k, i))
+                toks = slice(i * P, (i + 1) * P)
+                nc.tensor.matmul_mx(
+                    out=banks[("f", k, i)][:],
+                    lhsT=h_codes[:, k, toks].bitcast(FP8X4),
+                    lhsT_scale=h_scales[:, k, toks],
+                    rhs=w2_codes[:].bitcast(FP8X4),
+                    rhs_scale=w2_scales[:],
+                    start=True,
+                    stop=True,
+                )
 
-        def dm():
-            if "dm" not in banks:
-                banks["dm"] = psum.tile([P, 512], F32, tag="dm", bufs=1, name="dmb")
-            nc.tensor.matmul_mx(
-                out=banks["dm"][:],
-                lhsT=dcod[:, 0:P].bitcast(FP8X4),
-                lhsT_scale=dsca[:, 0:P],
-                rhs=dcod[:].bitcast(FP8X4),
-                rhs_scale=dsca[:],
-                start=True,
-                stop=True,
-            )
-
-        def addb(k, t):
-            i = 2 * k + t
+        def add_bias(k, i):
+            first = LEAD + WIDTH * (2 * k + i)
             nc.vector.tensor_tensor(
-                out=o_sb[:, SHIFT + O * i : SHIFT + O * (i + 1)], in0=banks[("l2", k, t)][:], in1=b2bc[:], op=ALU.add
+                out=out_sb[:, first : first + WIDTH], in0=banks[("f", k, i)][:], in1=bias_all[:], op=ALU.add
             )
 
-        def sqr(k):
-            nc.scalar.activation(out=sq[k][:], in_=oc(k)[:, :, 7:11], func=ACT.Square)
+        def tanh_and_squares(k):
+            nc.scalar.activation(out=squares[k][:], in_=channels(k)[:, :, 7:11], func=ACT.Square)
+            nc.scalar.activation(out=tanh_sb[k][:], in_=channels(k)[:, :, 0:7], func=ACT.Tanh, scale=0.5)
 
-        def red(k):
-            nc.vector.tensor_reduce(out=ss[:, 64 * k : 64 * k + 64], in_=sq[k][:], axis=AX.X, op=ALU.add)
+        def sum_squares(k):
+            nc.vector.tensor_reduce(
+                out=norm2[:, k * ROWS : (k + 1) * ROWS], in_=squares[k][:], axis=mybir.AxisListType.X, op=ALU.add
+            )
 
-        def th(k):
-            nc.scalar.activation(out=tht[k][:], in_=oc(k)[:, :, 0:7], func=ACT.Tanh, scale=0.5)
+        def inverse_norms(pair):
+            cols = slice(2 * pair * ROWS, 2 * (pair + 1) * ROWS)
+            nc.scalar.activation(out=inv_norm[:, cols], in_=norm2[:, cols], func=ACT.Abs_reciprocal_sqrt)
 
-        def clip(k):
+        def colours(k):
             nc.vector.tensor_scalar(
-                out=oc(k)[:, :, 11:16], in0=oc(k)[:, :, 11:16], scalar1=0.0, scalar2=1.0, op0=ALU.max, op1=ALU.min
+                out=channels(k)[:, :, 11:16], in0=channels(k)[:, :, 11:16],
+                scalar1=0.0, scalar2=1.0, op0=ALU.max, op1=ALU.min,
             )
 
-        def opc(k):
+        def means(k):
             nc.vector.scalar_tensor_tensor(
-                out=oc(k)[:, :, 0:3], in0=tht[k][:, :, 0:3], scalar=0.1,
-                in1=a3x[:, 2 * k : 2 * k + 2].rearrange("p i g c -> p (i g) c"),
+                out=channels(k)[:, :, 0:3], in0=tanh_sb[k][:, :, 0:3], scalar=0.1,
+                in1=centre[:, 2 * k : 2 * k + 2].rearrange("p i g c -> p (i g) c"),
                 op0=ALU.mult, op1=ALU.add,
             )
 
-        def opd(k):
+        def opacity_and_sizes(k):
             nc.vector.scalar_tensor_tensor(
-                out=oc(k)[:, :, 3:7], in0=tht[k][:, :, 3:7], scalar=1.0,
-                in1=s4[:].unsqueeze(1).to_broadcast([P, 2 * NG, 4]),
+                out=channels(k)[:, :, 3:7], in0=tanh_sb[k][:, :, 3:7], scalar=1.0,
+                in1=half_scale[:].unsqueeze(1).to_broadcast([P, ROWS, 4]),
                 op0=ALU.add, op1=ALU.mult,
             )
 
-        def sqrt(b):
-            lo, hi = BATCH[b]
-            nc.scalar.activation(out=rn[:, lo:hi], in_=ss[:, lo:hi], func=ACT.Abs_reciprocal_sqrt)
-
-        def opj(k):
+        def rotations_and_store(k):
             nc.vector.scalar_tensor_tensor(
-                out=oc(k)[:, :, 7:11],
-                in0=rn[:, 64 * k : 64 * k + 64].unsqueeze(2).to_broadcast([P, 2 * NG, 4]),
-                scalar=1e12, in1=oc(k)[:, :, 7:11], op0=ALU.min, op1=ALU.mult,
+                out=channels(k)[:, :, 7:11],
+                in0=inv_norm[:, k * ROWS : (k + 1) * ROWS].unsqueeze(2).to_broadcast([P, ROWS, 4]),
+                scalar=1e12, in1=channels(k)[:, :, 7:11], op0=ALU.min, op1=ALU.mult,
             )
-
-        def st(k):
+            first = LEAD + 2 * WIDTH * k
             nc.sync.dma_start(
                 out=out_v[:, 2 * k : 2 * k + 2, :],
-                in_=o_sb[:, SHIFT + 2 * O * k : SHIFT + 2 * O * (k + 1)].rearrange("p (i f) -> p i f", i=2),
+                in_=out_sb[:, first : first + 2 * WIDTH].rearrange("p (i f) -> p i f", i=2),
             )
 
-        fns = {
-            "rgW1v": rgW1v, "rgW1s": rgW1s, "qW1": qW1, "rgW2": rgW2, "qW2": qW2, "tr": tr, "cp": cp, "ql": ql,
-            "l1": l1, "si": si, "rg": rg, "qh": qh, "l2": l2, "A": addb, "sq": sqr, "red": red, "th": th,
-            "clip": clip, "C": opc, "D": opd, "sqrt": sqrt, "J": opj, "st": st, "b2c": b2c, "b1f": b1c, "pb": pbm, "dm": dm,
-        }
-        for item in ORDER:
-            fns[item[0]](*item[1:])
+        for g in range(2):
+            regroup_w1_vector(g)
+            regroup_w1_scalar(g)
+        for g in range(2):
+            quantise_w1(g)
+        nc.scalar.copy(out=b1_f32[:], in_=b1_sb[:])
+        for k in (0, 1):
+            transpose_latents(k)
+            copy_latents(k)
+        spread_bias()
+        quantise_latents(0)
+        regroup_w2()
+        quantise_latents(1)
+
+        for s in range(CHUNKS + 3):
+            if s < CHUNKS:
+                layer1(s)
+                silu(s)
+            if 1 <= s <= CHUNKS:
+                layer2(s - 1)
+            if s + 2 < CHUNKS:
+                transpose_latents(s + 2)
+                copy_latents(s + 2)
+            if s == 0:
+                nc.scalar.copy(out=bias_all[:], in_=banks["bias"][:])
+            if 2 <= s < CHUNKS + 2:
+                tanh_and_squares(s - 2)
+
+            if 1 <= s <= CHUNKS:
+                add_bias(s - 1, 0)
+            if s < CHUNKS:
+                regroup_h(s)
+            if s == 0:
+                quantise_w2()
+            if 1 <= s <= CHUNKS:
+                add_bias(s - 1, 1)
+            if s < CHUNKS:
+                quantise_h(s)
+            if s + 2 < CHUNKS:
+                quantise_latents(s + 2)
+            if s >= 4 and s % 2 == 0:
+                rotations_and_store(s - 4)
+                rotations_and_store(s - 3)
+            if 2 <= s < CHUNKS + 2:
+                sum_squares(s - 2)
+                if s % 2 == 1:
+                    inverse_norms((s - 3) // 2)
+                colours(s - 2)
+                means(s - 2)
+                opacity_and_sizes(s - 2)

@@ -148,6 +148,12 @@ def tile_gaussianrenderer_kernel(tc, xyzs, latents, W1, b1, W2, b2, out):
                 start=True, stop=True,
             )
 
+        def keep_clock_up(count):
+            if "idle" not in banks:
+                banks["idle"] = psum.tile([P, WIDTH], F32, tag="hT", bufs=2, name="idle_bank")
+            for j in range(count):
+                nc.tensor.matmul(out=banks["idle"][:], lhsT=ones[:], rhs=w1_raw[:, 0, 0:WIDTH], start=True, stop=True)
+
         def transpose_latents(k):
             for g in range(2):
                 bank = psum.tile([P, 2, CHUNK], F32, tag="latT", bufs=4, name="latT%d%d" % (k, g))
@@ -275,9 +281,11 @@ def tile_gaussianrenderer_kernel(tc, xyzs, latents, W1, b1, W2, b2, out):
         for g in range(2):
             quantise_w1(g)
         nc.scalar.copy(out=b1_f32[:], in_=b1_sb[:])
+        keep_clock_up(4)
         for k in (0, 1):
             transpose_latents(k)
             copy_latents(k)
+            keep_clock_up(2)
         spread_bias()
         quantise_latents(0)
         regroup_w2()

@@ -24,6 +24,11 @@ ROWS = 2 * GAUSS
 GROUPS = WIDTH // P
 W1_VECTOR_COLS = 384
 LEAD = 1
+VLAT = (1, 5, 7)
+BL = "CDEFCDEF"
+BT = "EFEF"
+BF_ = "CDCD"
+BB = "ABAB"
 
 FLOPS = 2 * TOKENS * K1 * WIDTH + 2 * TOKENS * WIDTH * WIDTH
 
@@ -49,25 +54,30 @@ def tile_gaussianrenderer_kernel(tc, xyzs, latents, W1, b1, W2, b2, out):
         psum = ctx.enter_context(tc.psum_pool(name="psum", bufs=2))
 
         xyz_sb = keep.tile([P, TILES, 3], BF16)
-        b1_sb = keep.tile([P, GROUPS], BF16)
+        b_row = keep.tile([1, 2 * WIDTH], BF16)
+        b1_rows = keep.tile([P, WIDTH], BF16)
         bias_rows = keep.tile([P, GAUSS, CH], BF16)
+        b2_rows = keep.tile([P, 3, 4, GAUSS], BF16)
         w1_raw = keep.tile([P, 4, 2 * WIDTH], BF16)
         lat_sb = keep.tile([P, TILES, K1], BF16)
         w2_raw = keep.tile([P, 4, WIDTH], BF16)
 
-        nc.sync.dma_start(out=xyz_sb[:], in_=xyz_v)
-        with nc.allow_non_contiguous_dma(reason="b1[128 m + p] goes to partition p, column m"):
-            nc.scalar.dma_start(out=b1_sb[:], in_=b1.rearrange("(m p) -> p m", p=P))
-        nc.vector.memset(bias_rows[:], 0.0)
+        nc.scalar.dma_start(out=b_row[:, WIDTH : 2 * WIDTH], in_=b2.unsqueeze(0))
+        nc.scalar.dma_start(out=b_row[:, 0:WIDTH], in_=b1.unsqueeze(0))
+        nc.scalar.dma_start(out=xyz_sb[:], in_=xyz_v)
+        nc.vector.memset(bias_rows[:].rearrange("p g c -> p (g c)").bitcast(U32), 0)
+        nc.vector.memset(b1_rows[:].bitcast(U32), 0)
+        nc.vector.memset(b2_rows[:].rearrange("p a j g -> p (a j g)").bitcast(U32), 0)
         nc.vector.memset(bias_rows[32:33, :, 11:16], 0.5)
-        nc.scalar.dma_start(out=bias_rows[0:1].rearrange("o g c -> o (g c)"), in_=b2.unsqueeze(0))
         for g in range(2):
             nc.sync.dma_start(out=w1_raw[:, 2 * g : 2 * g + 2, :], in_=w1_v[:, 2 * g : 2 * g + 2, :])
-        for k in (0, 1):
-            nc.sync.dma_start(out=lat_sb[:, 2 * k : 2 * k + 2, :], in_=lat_v[:, 2 * k : 2 * k + 2, :])
+        nc.sync.dma_start(out=lat_sb[:, 0, :], in_=lat_v[:, 0, :])
+        nc.sync.dma_start(out=lat_sb[:, 1, :], in_=lat_v[:, 1, :])
+        nc.sync.dma_start(out=lat_sb[:, 2, :], in_=lat_v[:, 2, :])
+        nc.sync.dma_start(out=lat_sb[:, 3, :], in_=lat_v[:, 3, :])
         nc.sync.dma_start(out=w2_raw[:], in_=w2_v)
-        for k in (2, 3):
-            nc.sync.dma_start(out=lat_sb[:, 2 * k : 2 * k + 2, :], in_=lat_v[:, 2 * k : 2 * k + 2, :])
+        nc.sync.dma_start(out=lat_sb[:, 4 : 6, :], in_=lat_v[:, 4 : 6, :])
+        nc.sync.dma_start(out=lat_sb[:, 6 : 8, :], in_=lat_v[:, 6 : 8, :])
 
         warm = keep.tile([P, 1], F32)
         nc.vector.memset(warm[:], 0.0)
@@ -83,14 +93,25 @@ def tile_gaussianrenderer_kernel(tc, xyzs, latents, W1, b1, W2, b2, out):
                 out=half_scale[:, cols], in0=half_scale[:, cols],
                 scalar1=factor, scalar2=0.0, op0=ALU.mult, op1=ALU.add,
             )
+        b2_by_channel = b_row[:, WIDTH : 2 * WIDTH].rearrange("o (g c) -> o c g", c=CH)
+        for dst, values, factor in (
+            (b2_rows[0:1, 0, 1:4], b2_by_channel[:, 0:3], 0.5),
+            (b2_rows[0:1, 1], b2_by_channel[:, 3:7], 0.5),
+            (b2_rows[0:1, 2], b2_by_channel[:, 7:11], 1.0),
+            (b1_rows[0:1], b_row[:, 0:WIDTH], 1.0),
+            (bias_rows[0:1].rearrange("o g c -> o (g c)"), b_row[:, WIDTH : 2 * WIDTH], 1.0),
+        ):
+            nc.gpsimd.tensor_scalar(out=dst, in0=values, scalar1=factor, scalar2=0.0, op0=ALU.mult, op1=ALU.add)
         centre = keep.tile([P, TILES, GAUSS, 3], F32)
         nc.gpsimd.tensor_scalar(
             out=centre[:], in0=xyz_sb[:].unsqueeze(2).to_broadcast([P, TILES, GAUSS, 3]),
             scalar1=1.0, scalar2=0.1, op0=ALU.mult, op1=ALU.add,
         )
 
-        b1_f32 = keep.tile([P, GROUPS], F32)
-        bias_all = keep.tile([P, WIDTH], F32)
+        bias_cols = keep.tile([P, GROUPS + 3], F32)
+        bias_8 = keep.tile([P, GAUSS, 8], F32)
+        bias_15 = keep.tile([P, GAUSS], F32)
+        same_gauss = keep.tile([P, GAUSS], F32)
         w1_grouped = [keep.tile([P, WIDTH, 4], BF16, align_bytes=64, name="w1_grouped%d" % g) for g in range(2)]
         w1_codes = keep.tile([P, 2, WIDTH], U32, align_bytes=64)
         w1_scales = keep.tile([P, 2, WIDTH], U8, align_bytes=64)
@@ -105,15 +126,23 @@ def tile_gaussianrenderer_kernel(tc, xyzs, latents, W1, b1, W2, b2, out):
         h_codes = keep.tile([P, CHUNKS, CHUNK], U32, align_bytes=64)
         h_scales = keep.tile([P, CHUNKS, CHUNK], U8, align_bytes=64)
         out_sb = keep.tile([P, TILES * WIDTH + 4], F32)
-        tanh_sb = [keep.tile([P, ROWS, 7], F32, name="tanh_sb%d" % k) for k in range(CHUNKS)]
-        squares = [keep.tile([P, ROWS, 4], F32, name="squares%d" % k) for k in range(CHUNKS)]
-        norm2 = keep.tile([P, CHUNKS * ROWS], F32)
+        tanh_t = [keep.tile([P, 2, CHUNK], F32, name="tanh_t%d" % k) for k in range(CHUNKS)]
+        squares_t = [keep.tile([P, CHUNK], F32, name="squares_t%d" % k) for k in range(CHUNKS)]
+        last_colour = keep.tile([P, TILES, GAUSS], F32)
         inv_norm = keep.tile([P, CHUNKS * ROWS], F32)
         banks = {}
 
         def channels(k):
             first = LEAD + 2 * WIDTH * k
+            return out_sb[:, first : first + 2 * WIDTH].rearrange("p (i g c) -> p i g c", i=2, c=CH)
+
+        def gaussians(k):
+            first = LEAD + 2 * WIDTH * k
             return out_sb[:, first : first + 2 * WIDTH].rearrange("p (r c) -> p r c", c=CH)
+
+        def bank_tile(key, bank, shape):
+            banks[key] = psum.tile(shape, F32, tag=bank, bufs=1, name="bank%s" % bank)
+            return banks[key]
 
         def w1_rows(g):
             return w1_raw[:, 2 * g : 2 * g + 2, :].rearrange("p u (e c) -> p (u e) c", e=2)
@@ -133,8 +162,13 @@ def tile_gaussianrenderer_kernel(tc, xyzs, latents, W1, b1, W2, b2, out):
             )
 
         def regroup_w2():
-            dst, src = side_by_side(w2_grouped[:], w2_raw[:])
-            nc.vector.tensor_copy(out=dst, in_=src)
+            dst = w2_grouped[:].rearrange("p (s g) t -> p g s t", g=GAUSS)
+            src = w2_raw[:].rearrange("p t (g c) -> p g c t", c=CH)
+            for chan, count in ((0, 3), (3, 4), (7, 4), (11, 4)):
+                nc.vector.tensor_copy(
+                    out=dst[:, :, chan + 1 : chan + 1 + count], in_=src[:, :, chan : chan + count]
+                )
+            nc.vector.tensor_copy(out=dst[:, :, 0], in_=src[:, :, 15])
 
         def quantise_w2():
             nc.vector.quantize_mx(
@@ -142,34 +176,52 @@ def tile_gaussianrenderer_kernel(tc, xyzs, latents, W1, b1, W2, b2, out):
             )
 
         def spread_bias():
-            banks["bias"] = psum.tile([P, WIDTH], F32, tag="f", bufs=2, name="bias_bank")
+            bank = bank_tile("bias", "G", [P, WIDTH])
             nc.tensor.matmul(
-                out=banks["bias"][:], lhsT=ones[:], rhs=bias_rows[:].rearrange("p g c -> p (g c)"),
+                out=bank[:], lhsT=ones[:], rhs=bias_rows[:].rearrange("p g c -> p (g c)"),
                 start=True, stop=True,
             )
 
+        def columns_of_biases():
+            bank = bank_tile("bias cols", "N", [P, WIDTH])
+            b2_cols = b2_rows[:].rearrange("p a j g -> p (a j g)")
+            for m in range(GROUPS + 3):
+                rows, first = (b1_rows[:], m * P) if m < GROUPS else (b2_cols, (m - GROUPS) * P)
+                nc.tensor.matmul(
+                    out=bank[:, m : m + 1], lhsT=rows[:, first : first + P], rhs=ones[:, 0:1], start=True, stop=True
+                )
+
         def keep_clock_up(count):
             if "idle" not in banks:
-                banks["idle"] = psum.tile([P, WIDTH], F32, tag="hT", bufs=2, name="idle_bank")
+                bank_tile("idle", "A", [P, WIDTH])
             for j in range(count):
                 nc.tensor.matmul(out=banks["idle"][:], lhsT=ones[:], rhs=w1_raw[:, 0, 0:WIDTH], start=True, stop=True)
 
         def transpose_latents(k):
+            for i in range(2):
+                transpose_tile(2 * k + i)
+
+        def transpose_tile(i):
+            bank = bank_tile(("latT", i), BL[i], [P, 2, 2, P])
+            words = lat_sb[:, i, :].bitcast(F32)
             for g in range(2):
-                bank = psum.tile([P, 2, CHUNK], F32, tag="latT", bufs=4, name="latT%d%d" % (k, g))
-                banks[("latT", k, g)] = bank
-                for i in range(2):
-                    words = lat_sb[:, 2 * k + i, :].bitcast(F32)
-                    for u in range(2):
-                        first = 256 * g + 128 * u
-                        nc.tensor.transpose(
-                            out=bank[:, u, i * P : (i + 1) * P], in_=words[:, first : first + P], identity=ident[:]
-                        )
+                for u in range(2):
+                    first = 256 * g + 128 * u
+                    nc.tensor.transpose(out=bank[:, g, u, :], in_=words[:, first : first + P], identity=ident[:])
 
         def copy_latents(k):
-            grouped = lat_grouped[k][:].bitcast(F32).rearrange("p (g n u) -> p g n u", g=2, u=2)
-            for g in range(2):
-                nc.scalar.copy(out=grouped[:, g], in_=banks[("latT", k, g)][:].rearrange("p u n -> p n u"))
+            for i in range(2):
+                copy_tile(2 * k + i)
+
+        def copy_tile(i):
+            grouped = lat_grouped[i // 2][:].bitcast(F32).rearrange("p (g n u) -> p g n u", g=2, u=2)
+            toks = slice((i % 2) * P, (i % 2 + 1) * P)
+            out = grouped[:, :, toks]
+            src = banks[("latT", i)][:].rearrange("p g u n -> p g n u")
+            if i in VLAT:
+                nc.vector.tensor_copy(out=out, in_=src)
+            else:
+                nc.scalar.copy(out=out, in_=src)
 
         def quantise_latents(k):
             nc.vector.quantize_mx(
@@ -179,7 +231,7 @@ def tile_gaussianrenderer_kernel(tc, xyzs, latents, W1, b1, W2, b2, out):
         def layer1(k):
             for m in range(GROUPS):
                 if m % 2 == 0:
-                    banks[("hT", k, m // 2)] = psum.tile([P, 2, CHUNK], F32, tag="hT", bufs=2, name="hT%d%d" % (k, m // 2))
+                    bank_tile(("hT", k, m // 2), "AB"[m // 2], [P, 2, CHUNK])
                 cols = slice(m * P, (m + 1) * P)
                 for g in range(2):
                     toks = slice(g * CHUNK, (g + 1) * CHUNK)
@@ -197,7 +249,7 @@ def tile_gaussianrenderer_kernel(tc, xyzs, latents, W1, b1, W2, b2, out):
             for m in range(GROUPS):
                 nc.scalar.activation(
                     out=h_planes[k][:, m, :], in_=banks[("hT", k, m // 2)][:, m % 2, :],
-                    func=ACT.Silu, bias=b1_f32[:, m : m + 1], scale=1.0,
+                    func=ACT.Silu, bias=bias_cols[:, m : m + 1], scale=1.0,
                 )
 
         def regroup_h(k):
@@ -210,120 +262,228 @@ def tile_gaussianrenderer_kernel(tc, xyzs, latents, W1, b1, W2, b2, out):
                 in_=h_grouped[k][:].rearrange("p n t -> p (n t)"),
             )
 
-        def layer2(k):
+        def layer2_transposed(k, a, out):
+            cols = slice(a * P, (a + 1) * P)
+            nc.tensor.matmul_mx(
+                out=out, lhsT=w2_codes[:, cols].bitcast(FP8X4), lhsT_scale=w2_scales[:, cols],
+                rhs=h_codes[:, k, :].bitcast(FP8X4), rhs_scale=h_scales[:, k, :], start=True, stop=True,
+            )
+
+        def layer2_tokens(i, cols, out):
+            toks = slice((i % 2) * P, (i % 2 + 1) * P)
+            nc.tensor.matmul_mx(
+                out=out, lhsT=h_codes[:, i // 2, toks].bitcast(FP8X4), lhsT_scale=h_scales[:, i // 2, toks],
+                rhs=w2_codes[:, cols].bitcast(FP8X4), rhs_scale=w2_scales[:, cols], start=True, stop=True,
+            )
+
+        def layer2_rotations(k):
+            layer2_transposed(k, 2, bank_tile(("rot", k), "G", [P, CHUNK])[:])
+
+        def layer2_tanh(k):
+            bank = bank_tile(("tanh", k), BT[k], [P, 2, CHUNK])
+            for a in range(2):
+                layer2_transposed(k, a, bank[:, a, :])
+
+        def layer2_rest(k):
+            bank = bank_tile(("f", k), BF_[k], [P, 2, 2 * P])
             for i in range(2):
-                banks[("f", k, i)] = psum.tile([P, WIDTH], F32, tag="f", bufs=2, name="f%d%d" % (k, i))
-                toks = slice(i * P, (i + 1) * P)
-                nc.tensor.matmul_mx(
-                    out=banks[("f", k, i)][:],
-                    lhsT=h_codes[:, k, toks].bitcast(FP8X4),
-                    lhsT_scale=h_scales[:, k, toks],
-                    rhs=w2_codes[:].bitcast(FP8X4),
-                    rhs_scale=w2_scales[:],
-                    start=True,
-                    stop=True,
+                layer2_tokens(2 * k + i, slice(2 * P, 4 * P), bank[:, i, :])
+
+        def layer2_last_colour():
+            bank = bank_tile("last", "G", [P, TILES, 64])
+            for i in range(TILES):
+                layer2_tokens(i, slice(0, 64), bank[:, i, :])
+
+        def tanh(k):
+            for a in range(2):
+                nc.scalar.activation(
+                    out=tanh_t[k][:, a, :], in_=banks[("tanh", k)][:, a, :],
+                    func=ACT.Tanh, bias=bias_cols[:, GROUPS + a : GROUPS + a + 1], scale=0.5,
                 )
 
-        def add_bias(k, i):
-            first = LEAD + WIDTH * (2 * k + i)
-            nc.vector.tensor_tensor(
-                out=out_sb[:, first : first + WIDTH], in0=banks[("f", k, i)][:], in1=bias_all[:], op=ALU.add
+        def squares(k):
+            nc.scalar.activation(
+                out=squares_t[k][:], in_=banks[("rot", k)][:],
+                func=ACT.Square, bias=bias_cols[:, GROUPS + 2 : GROUPS + 3], scale=1.0,
             )
-
-        def tanh_and_squares(k):
-            nc.scalar.activation(out=squares[k][:], in_=channels(k)[:, :, 7:11], func=ACT.Square)
-            nc.scalar.activation(out=tanh_sb[k][:], in_=channels(k)[:, :, 0:7], func=ACT.Tanh, scale=0.5)
 
         def sum_squares(k):
-            nc.vector.tensor_reduce(
-                out=norm2[:, k * ROWS : (k + 1) * ROWS], in_=squares[k][:], axis=mybir.AxisListType.X, op=ALU.add
+            if k == 0:
+                bank_tile("norm", "N", [P, CHUNKS * ROWS])
+            for i in range(2):
+                first = (2 * k + i) * GAUSS
+                nc.tensor.matmul(
+                    out=banks["norm"][:, first : first + GAUSS], lhsT=squares_t[k][:, i * P : (i + 1) * P],
+                    rhs=same_gauss[:], start=True, stop=True,
+                )
+
+        def turn_tanh(k):
+            bank = bank_tile(("tanh back", k), BB[k], [P, 8, 2, GAUSS])
+            for i in range(2):
+                for a in range(2):
+                    nc.tensor.transpose(
+                        out=bank[:, 4 * a : 4 * a + 4, i, :], in_=tanh_t[k][:, a, i * P : (i + 1) * P], identity=ident[:]
+                    )
+
+        def tanh_back(k, slots):
+            return banks[("tanh back", k)][:, slots].rearrange("p s i g -> p (i g) s")
+
+        def add_bias(k):
+            nc.vector.tensor_tensor(
+                out=channels(k)[:, :, :, 7:15],
+                in0=banks[("f", k)][:].rearrange("p i (s g) -> p i g s", g=GAUSS),
+                in1=bias_8[:].unsqueeze(1).to_broadcast([P, 2, GAUSS, 8]), op=ALU.add,
             )
 
-        def inverse_norms(pair):
-            cols = slice(2 * pair * ROWS, 2 * (pair + 1) * ROWS)
-            nc.scalar.activation(out=inv_norm[:, cols], in_=norm2[:, cols], func=ACT.Abs_reciprocal_sqrt)
+        def add_bias_last_colour():
+            nc.vector.tensor_tensor(
+                out=last_colour[:], in0=banks["last"][:, :, 0:GAUSS],
+                in1=bias_15[:].unsqueeze(1).to_broadcast([P, TILES, GAUSS]), op=ALU.add,
+            )
+
+        def inverse_norms():
+            nc.scalar.activation(out=inv_norm[:], in_=banks["norm"][:], func=ACT.Abs_reciprocal_sqrt)
 
         def colours(k):
             nc.vector.tensor_scalar(
-                out=channels(k)[:, :, 11:16], in0=channels(k)[:, :, 11:16],
+                out=gaussians(k)[:, :, 11:15], in0=gaussians(k)[:, :, 11:15],
                 scalar1=0.0, scalar2=1.0, op0=ALU.max, op1=ALU.min,
+            )
+
+        def clip_last_colour():
+            nc.vector.tensor_scalar(
+                out=out_sb[:, LEAD : LEAD + TILES * WIDTH].rearrange("p (i g c) -> p i g c", i=TILES, c=CH)[:, :, :, 15],
+                in0=last_colour[:], scalar1=0.0, scalar2=1.0, op0=ALU.max, op1=ALU.min,
             )
 
         def means(k):
             nc.vector.scalar_tensor_tensor(
-                out=channels(k)[:, :, 0:3], in0=tanh_sb[k][:, :, 0:3], scalar=0.1,
-                in1=centre[:, 2 * k : 2 * k + 2].rearrange("p i g c -> p (i g) c"),
-                op0=ALU.mult, op1=ALU.add,
+                out=gaussians(k)[:, :, 0:3], in0=tanh_back(k, slice(1, 4)), scalar=0.1,
+                in1=centre[:, 2 * k : 2 * k + 2].rearrange("p i g c -> p (i g) c"), op0=ALU.mult, op1=ALU.add,
             )
 
         def opacity_and_sizes(k):
             nc.vector.scalar_tensor_tensor(
-                out=channels(k)[:, :, 3:7], in0=tanh_sb[k][:, :, 3:7], scalar=1.0,
+                out=gaussians(k)[:, :, 3:7], in0=tanh_back(k, slice(4, 8)), scalar=1.0,
                 in1=half_scale[:].unsqueeze(1).to_broadcast([P, ROWS, 4]),
                 op0=ALU.add, op1=ALU.mult,
             )
 
         def rotations_and_store(k):
+            rotations(k)
+            store(k)
+
+        def rotations(k):
+            inverse = inv_norm[:, k * ROWS : (k + 1) * ROWS]
             nc.vector.scalar_tensor_tensor(
-                out=channels(k)[:, :, 7:11],
-                in0=inv_norm[:, k * ROWS : (k + 1) * ROWS].unsqueeze(2).to_broadcast([P, ROWS, 4]),
-                scalar=1e12, in1=channels(k)[:, :, 7:11], op0=ALU.min, op1=ALU.mult,
+                out=gaussians(k)[:, :, 7:11], in0=inverse.unsqueeze(2).to_broadcast([P, ROWS, 4]),
+                scalar=1e12, in1=gaussians(k)[:, :, 7:11], op0=ALU.min, op1=ALU.mult,
             )
+
+        def store(k):
             first = LEAD + 2 * WIDTH * k
             nc.sync.dma_start(
                 out=out_v[:, 2 * k : 2 * k + 2, :],
                 in_=out_sb[:, first : first + 2 * WIDTH].rearrange("p (i f) -> p i f", i=2),
             )
 
+        nc.vector.tensor_reduce(
+            out=same_gauss[:], in_=ident[:].rearrange("p (j g) -> p g j", g=GAUSS), axis=mybir.AxisListType.X, op=ALU.add
+        )
+        keep_clock_up(3)
         for g in range(2):
             regroup_w1_vector(g)
             regroup_w1_scalar(g)
-        for g in range(2):
-            quantise_w1(g)
-        nc.scalar.copy(out=b1_f32[:], in_=b1_sb[:])
-        keep_clock_up(4)
-        for k in (0, 1):
-            transpose_latents(k)
-            copy_latents(k)
-            keep_clock_up(2)
+        columns_of_biases()
+        nc.scalar.copy(out=bias_cols[:], in_=banks["bias cols"][:, 0 : GROUPS + 3])
+        transpose_latents(0)
         spread_bias()
+        spread = banks["bias"][:].rearrange("p (g c) -> p g c", c=CH)
+        transpose_latents(1)
+        quantise_w1(0)
+        copy_tile(1)
+        quantise_w1(1)
+        copy_tile(0)
+        nc.scalar.copy(out=bias_8[:], in_=spread[:, :, 7:15])
+        nc.scalar.copy(out=bias_15[:], in_=spread[:, :, 15])
+        copy_tile(2)
+        copy_tile(3)
         quantise_latents(0)
-        regroup_w2()
         quantise_latents(1)
-
-        for s in range(CHUNKS + 3):
-            if s < CHUNKS:
-                layer1(s)
-                silu(s)
-            if 1 <= s <= CHUNKS:
-                layer2(s - 1)
-            if s + 2 < CHUNKS:
-                transpose_latents(s + 2)
-                copy_latents(s + 2)
-            if s == 0:
-                nc.scalar.copy(out=bias_all[:], in_=banks["bias"][:])
-            if 2 <= s < CHUNKS + 2:
-                tanh_and_squares(s - 2)
-
-            if 1 <= s <= CHUNKS:
-                add_bias(s - 1, 0)
-            if s < CHUNKS:
-                regroup_h(s)
-            if s == 0:
-                quantise_w2()
-            if 1 <= s <= CHUNKS:
-                add_bias(s - 1, 1)
-            if s < CHUNKS:
-                quantise_h(s)
-            if s + 2 < CHUNKS:
-                quantise_latents(s + 2)
-            if s >= 4 and s % 2 == 0:
-                rotations_and_store(s - 4)
-                rotations_and_store(s - 3)
-            if 2 <= s < CHUNKS + 2:
-                sum_squares(s - 2)
-                if s % 2 == 1:
-                    inverse_norms((s - 3) // 2)
-                colours(s - 2)
-                means(s - 2)
-                opacity_and_sizes(s - 2)
+        regroup_w2()
+        layer1(0)
+        silu(0)
+        transpose_latents(2)
+        transpose_latents(3)
+        copy_tile(4)
+        copy_tile(5)
+        copy_tile(6)
+        quantise_w2()
+        quantise_latents(2)
+        copy_tile(7)
+        layer1(1)
+        silu(1)
+        regroup_h(0)
+        quantise_latents(3)
+        layer1(2)
+        silu(2)
+        regroup_h(1)
+        quantise_h(0)
+        layer1(3)
+        silu(3)
+        layer2_rotations(0)
+        layer2_tanh(0)
+        layer2_rest(0)
+        squares(0)
+        tanh(0)
+        regroup_h(2)
+        quantise_h(1)
+        layer2_tanh(1)
+        layer2_rotations(1)
+        sum_squares(0)
+        turn_tanh(0)
+        squares(1)
+        tanh(1)
+        quantise_h(2)
+        regroup_h(3)
+        add_bias(0)
+        layer2_rotations(2)
+        sum_squares(1)
+        layer2_rest(1)
+        squares(2)
+        quantise_h(3)
+        layer2_rotations(3)
+        sum_squares(2)
+        squares(3)
+        turn_tanh(1)
+        opacity_and_sizes(0)
+        means(0)
+        colours(0)
+        layer2_tanh(2)
+        layer2_rest(2)
+        sum_squares(3)
+        inverse_norms()
+        layer2_last_colour()
+        tanh(2)
+        add_bias(1)
+        layer2_tanh(3)
+        layer2_rest(3)
+        tanh(3)
+        opacity_and_sizes(1)
+        means(1)
+        colours(1)
+        add_bias_last_colour()
+        add_bias(2)
+        clip_last_colour()
+        rotations_and_store(0)
+        rotations_and_store(1)
+        add_bias(3)
+        colours(2)
+        rotations(2)
+        rotations(3)
+        colours(3)
+        for k in (2, 3):
+            turn_tanh(k)
+            opacity_and_sizes(k)
+            means(k)
+            store(k)

@@ -54,7 +54,6 @@ def tile_gaussianrenderer_kernel(tc, xyzs, latents, W1, b1, W2, b2, out):
         psum = ctx.enter_context(tc.psum_pool(name="psum", bufs=2))
 
         xyz_sb = keep.tile([P, TILES, 3], BF16)
-        b_row = keep.tile([1, 2 * WIDTH], BF16)
         b1_rows = keep.tile([P, WIDTH], BF16)
         bias_rows = keep.tile([P, GAUSS, CH], BF16)
         b2_rows = keep.tile([P, 3, 4, GAUSS], BF16)
@@ -62,13 +61,14 @@ def tile_gaussianrenderer_kernel(tc, xyzs, latents, W1, b1, W2, b2, out):
         lat_sb = keep.tile([P, TILES, K1], BF16)
         w2_raw = keep.tile([P, 4, WIDTH], BF16)
 
-        nc.scalar.dma_start(out=b_row[:, WIDTH : 2 * WIDTH], in_=b2.unsqueeze(0))
-        nc.scalar.dma_start(out=b_row[:, 0:WIDTH], in_=b1.unsqueeze(0))
+        b_row = keep.tile([1, 2, WIDTH], BF16)
+        nc.sync.dma_start(out=b_row[:, 0], in_=b1.unsqueeze(0))
+        nc.sync.dma_start(out=b_row[:, 1], in_=b2.unsqueeze(0))
         nc.scalar.dma_start(out=xyz_sb[:], in_=xyz_v)
         nc.vector.memset(bias_rows[:].rearrange("p g c -> p (g c)").bitcast(U32), 0)
         nc.vector.memset(b1_rows[:].bitcast(U32), 0)
-        nc.vector.memset(b2_rows[:].rearrange("p a j g -> p (a j g)").bitcast(U32), 0)
         nc.vector.memset(bias_rows[32:33, :, 11:16], 0.5)
+        nc.vector.memset(b2_rows[:].rearrange("p a j g -> p (a j g)").bitcast(U32), 0)
         for g in range(2):
             nc.sync.dma_start(out=w1_raw[:, 2 * g : 2 * g + 2, :], in_=w1_v[:, 2 * g : 2 * g + 2, :])
         nc.sync.dma_start(out=lat_sb[:, 0, :], in_=lat_v[:, 0, :])
@@ -93,20 +93,17 @@ def tile_gaussianrenderer_kernel(tc, xyzs, latents, W1, b1, W2, b2, out):
                 out=half_scale[:, cols], in0=half_scale[:, cols],
                 scalar1=factor, scalar2=0.0, op0=ALU.mult, op1=ALU.add,
             )
-        b2_by_channel = b_row[:, WIDTH : 2 * WIDTH].rearrange("o (g c) -> o c g", c=CH)
-        for dst, values, factor in (
-            (b2_rows[0:1, 0, 1:4], b2_by_channel[:, 0:3], 0.5),
-            (b2_rows[0:1, 1], b2_by_channel[:, 3:7], 0.5),
-            (b2_rows[0:1, 2], b2_by_channel[:, 7:11], 1.0),
-            (b1_rows[0:1], b_row[:, 0:WIDTH], 1.0),
-            (bias_rows[0:1].rearrange("o g c -> o (g c)"), b_row[:, WIDTH : 2 * WIDTH], 1.0),
-        ):
-            nc.gpsimd.tensor_scalar(out=dst, in0=values, scalar1=factor, scalar2=0.0, op0=ALU.mult, op1=ALU.add)
-        centre = keep.tile([P, TILES, GAUSS, 3], F32)
-        nc.gpsimd.tensor_scalar(
-            out=centre[:], in0=xyz_sb[:].unsqueeze(2).to_broadcast([P, TILES, GAUSS, 3]),
-            scalar1=1.0, scalar2=0.1, op0=ALU.mult, op1=ALU.add,
-        )
+        addend = keep.tile([P, 4, CHUNKS, ROWS + 2], F32)
+        nc.gpsimd.memset(addend[:, 0, :, 0:1], 0.0)
+        for c in range(3):
+            nc.gpsimd.tensor_scalar(
+                out=addend[:, 1 + c, :, 0:ROWS].rearrange("p k (i g) -> p k i g", g=GAUSS),
+                in0=xyz_sb[:, :, c].rearrange("p (k i) -> p k i", i=2).unsqueeze(3).to_broadcast([P, CHUNKS, 2, GAUSS]),
+                scalar1=1.0, scalar2=0.1, op0=ALU.mult, op1=ALU.add,
+            )
+        half_cols = keep.tile([P, 2], F32)
+        nc.gpsimd.memset(half_cols[:], 0.5)
+        nc.gpsimd.memset(half_cols[0:GAUSS, 0:1], 0.0)
 
         bias_cols = keep.tile([P, GROUPS + 3], F32)
         bias_8 = keep.tile([P, GAUSS, 8], F32)
@@ -125,7 +122,7 @@ def tile_gaussianrenderer_kernel(tc, xyzs, latents, W1, b1, W2, b2, out):
         h_grouped = [keep.tile([P, CHUNK, 4], BF16, align_bytes=64, name="h_grouped%d" % k) for k in range(CHUNKS)]
         h_codes = keep.tile([P, CHUNKS, CHUNK], U32, align_bytes=64)
         h_scales = keep.tile([P, CHUNKS, CHUNK], U8, align_bytes=64)
-        out_sb = keep.tile([P, TILES * WIDTH + 4], F32)
+        out_sb = keep.tile([P, CHUNKS, 2 * WIDTH + 4], F32)
         tanh_t = [keep.tile([P, 2, CHUNK], F32, name="tanh_t%d" % k) for k in range(CHUNKS)]
         squares_t = [keep.tile([P, CHUNK], F32, name="squares_t%d" % k) for k in range(CHUNKS)]
         last_colour = keep.tile([P, TILES, GAUSS], F32)
@@ -133,12 +130,10 @@ def tile_gaussianrenderer_kernel(tc, xyzs, latents, W1, b1, W2, b2, out):
         banks = {}
 
         def channels(k):
-            first = LEAD + 2 * WIDTH * k
-            return out_sb[:, first : first + 2 * WIDTH].rearrange("p (i g c) -> p i g c", i=2, c=CH)
+            return out_sb[:, k, LEAD : LEAD + 2 * WIDTH].rearrange("p (i g c) -> p i g c", i=2, c=CH)
 
         def gaussians(k):
-            first = LEAD + 2 * WIDTH * k
-            return out_sb[:, first : first + 2 * WIDTH].rearrange("p (r c) -> p r c", c=CH)
+            return out_sb[:, k, LEAD : LEAD + 2 * WIDTH].rearrange("p (r c) -> p r c", c=CH)
 
         def bank_tile(key, bank, shape):
             banks[key] = psum.tile(shape, F32, tag=bank, bufs=1, name="bank%s" % bank)
@@ -161,14 +156,11 @@ def tile_gaussianrenderer_kernel(tc, xyzs, latents, W1, b1, W2, b2, out):
                 in_=w1_grouped[g][:].rearrange("p c t -> p (c t)"),
             )
 
-        def regroup_w2():
+        def regroup_w2(chan, count, copy):
+            first = (chan + 1) % CH
             dst = w2_grouped[:].rearrange("p (s g) t -> p g s t", g=GAUSS)
             src = w2_raw[:].rearrange("p t (g c) -> p g c t", c=CH)
-            for chan, count in ((0, 3), (3, 4), (7, 4), (11, 4)):
-                nc.vector.tensor_copy(
-                    out=dst[:, :, chan + 1 : chan + 1 + count], in_=src[:, :, chan : chan + count]
-                )
-            nc.vector.tensor_copy(out=dst[:, :, 0], in_=src[:, :, 15])
+            copy(out=dst[:, :, first : first + count], in_=src[:, :, chan : chan + count])
 
         def quantise_w2():
             nc.vector.quantize_mx(
@@ -298,7 +290,7 @@ def tile_gaussianrenderer_kernel(tc, xyzs, latents, W1, b1, W2, b2, out):
             for a in range(2):
                 nc.scalar.activation(
                     out=tanh_t[k][:, a, :], in_=banks[("tanh", k)][:, a, :],
-                    func=ACT.Tanh, bias=bias_cols[:, GROUPS + a : GROUPS + a + 1], scale=0.5,
+                    func=ACT.Tanh, bias=bias_cols[:, GROUPS + a : GROUPS + a + 1], scale=half_cols[:, a : a + 1],
                 )
 
         def squares(k):
@@ -351,15 +343,20 @@ def tile_gaussianrenderer_kernel(tc, xyzs, latents, W1, b1, W2, b2, out):
             )
 
         def clip_last_colour():
+            last = addend[:, 0, :, 1 : ROWS + 1]
             nc.vector.tensor_scalar(
-                out=out_sb[:, LEAD : LEAD + TILES * WIDTH].rearrange("p (i g c) -> p i g c", i=TILES, c=CH)[:, :, :, 15],
-                in0=last_colour[:], scalar1=0.0, scalar2=1.0, op0=ALU.max, op1=ALU.min,
+                out=last, in0=last_colour[:].rearrange("p (k i) g -> p k (i g)", i=2),
+                scalar1=0.0, scalar2=1.0, op0=ALU.max, op1=ALU.min,
             )
+
+        def end_of_chunks():
+            nc.vector.tensor_copy(out=out_sb[:, :, 2 * WIDTH : 2 * WIDTH + 1], in_=addend[:, 0, :, ROWS : ROWS + 1])
 
         def means(k):
             nc.vector.scalar_tensor_tensor(
-                out=gaussians(k)[:, :, 0:3], in0=tanh_back(k, slice(1, 4)), scalar=0.1,
-                in1=centre[:, 2 * k : 2 * k + 2].rearrange("p i g c -> p (i g) c"), op0=ALU.mult, op1=ALU.add,
+                out=out_sb[:, k, 0 : 2 * WIDTH].rearrange("p (r c) -> p r c", c=CH)[:, :, 0:4],
+                in0=tanh_back(k, slice(0, 4)), scalar=0.1,
+                in1=addend[:, :, k, 0:ROWS].rearrange("p s r -> p r s"), op0=ALU.mult, op1=ALU.add,
             )
 
         def opacity_and_sizes(k):
@@ -381,36 +378,46 @@ def tile_gaussianrenderer_kernel(tc, xyzs, latents, W1, b1, W2, b2, out):
             )
 
         def store(k):
-            first = LEAD + 2 * WIDTH * k
             nc.sync.dma_start(
                 out=out_v[:, 2 * k : 2 * k + 2, :],
-                in_=out_sb[:, first : first + 2 * WIDTH].rearrange("p (i f) -> p i f", i=2),
+                in_=out_sb[:, k, LEAD : LEAD + 2 * WIDTH].rearrange("p (i f) -> p i f", i=2),
             )
 
         nc.vector.tensor_reduce(
             out=same_gauss[:], in_=ident[:].rearrange("p (j g) -> p g j", g=GAUSS), axis=mybir.AxisListType.X, op=ALU.add
         )
+        b2_by_channel = b_row[:, 1].rearrange("o (g c) -> o c g", c=CH)
+        nc.vector.tensor_copy(out=b1_rows[0:1], in_=b_row[:, 0])
+        nc.vector.tensor_scalar(
+            out=b2_rows[0:1].rearrange("o a j g -> o (a j) g")[:, 1:8], in0=b2_by_channel[:, 0:7],
+            scalar1=0.5, scalar2=0.0, op0=ALU.mult, op1=ALU.add,
+        )
+        nc.vector.tensor_copy(out=b2_rows[0:1, 2], in_=b2_by_channel[:, 7:11])
+        nc.vector.tensor_copy(out=bias_rows[0:1].rearrange("o g c -> o (g c)"), in_=b_row[:, 1])
         keep_clock_up(3)
-        for g in range(2):
-            regroup_w1_vector(g)
-            regroup_w1_scalar(g)
-        columns_of_biases()
-        nc.scalar.copy(out=bias_cols[:], in_=banks["bias cols"][:, 0 : GROUPS + 3])
-        transpose_latents(0)
-        spread_bias()
-        spread = banks["bias"][:].rearrange("p (g c) -> p g c", c=CH)
-        transpose_latents(1)
+        regroup_w1_vector(0)
+        regroup_w1_scalar(0)
         quantise_w1(0)
+        regroup_w1_vector(1)
+        regroup_w1_scalar(1)
+        transpose_latents(0)
         copy_tile(1)
         quantise_w1(1)
         copy_tile(0)
-        nc.scalar.copy(out=bias_8[:], in_=spread[:, :, 7:15])
-        nc.scalar.copy(out=bias_15[:], in_=spread[:, :, 15])
+        transpose_latents(1)
+        columns_of_biases()
+        spread_bias()
         copy_tile(2)
         copy_tile(3)
+        nc.scalar.copy(out=bias_cols[:], in_=banks["bias cols"][:, 0 : GROUPS + 3])
+        spread = banks["bias"][:].rearrange("p (g c) -> p g c", c=CH)
+        regroup_w2(11, 4, nc.scalar.copy)
         quantise_latents(0)
         quantise_latents(1)
-        regroup_w2()
+        regroup_w2(15, 1, nc.vector.tensor_copy)
+        regroup_w2(0, 1, nc.vector.tensor_copy)
+        for chan in range(1, 11, 2):
+            regroup_w2(chan, 2, nc.vector.tensor_copy)
         layer1(0)
         silu(0)
         transpose_latents(2)
@@ -423,6 +430,8 @@ def tile_gaussianrenderer_kernel(tc, xyzs, latents, W1, b1, W2, b2, out):
         copy_tile(7)
         layer1(1)
         silu(1)
+        nc.scalar.copy(out=bias_8[:], in_=spread[:, :, 7:15])
+        nc.scalar.copy(out=bias_15[:], in_=spread[:, :, 15])
         regroup_h(0)
         quantise_latents(3)
         layer1(2)
@@ -457,26 +466,29 @@ def tile_gaussianrenderer_kernel(tc, xyzs, latents, W1, b1, W2, b2, out):
         squares(3)
         turn_tanh(1)
         opacity_and_sizes(0)
-        means(0)
         colours(0)
         layer2_tanh(2)
         layer2_rest(2)
         sum_squares(3)
         inverse_norms()
-        layer2_last_colour()
         tanh(2)
+        layer2_last_colour()
         add_bias(1)
         layer2_tanh(3)
         layer2_rest(3)
         tanh(3)
         opacity_and_sizes(1)
-        means(1)
         colours(1)
-        add_bias_last_colour()
         add_bias(2)
+        add_bias_last_colour()
+        rotations(0)
         clip_last_colour()
-        rotations_and_store(0)
-        rotations_and_store(1)
+        rotations(1)
+        means(0)
+        end_of_chunks()
+        store(0)
+        means(1)
+        store(1)
         add_bias(3)
         colours(2)
         rotations(2)

@@ -24,11 +24,12 @@ ROWS = 2 * GAUSS
 GROUPS = WIDTH // P
 W1_VECTOR_COLS = 384
 LEAD = 1
-VLAT = (1, 5, 7)
+VLAT = (5, 7)
 BL = "CDEFCDEF"
-BT = "EFEF"
-BF_ = "CDCD"
-BB = "ABAB"
+BT = "EFCE"
+BF_ = "CDFD"
+BB = "ABFA"
+BR = "GGGE"
 
 FLOPS = 2 * TOKENS * K1 * WIDTH + 2 * TOKENS * WIDTH * WIDTH
 
@@ -269,7 +270,7 @@ def tile_gaussianrenderer_kernel(tc, xyzs, latents, W1, b1, W2, b2, out):
             )
 
         def layer2_rotations(k):
-            layer2_transposed(k, 2, bank_tile(("rot", k), "G", [P, CHUNK])[:])
+            layer2_transposed(k, 2, bank_tile(("rot", k), BR[k], [P, CHUNK])[:])
 
         def layer2_tanh(k):
             bank = bank_tile(("tanh", k), BT[k], [P, 2, CHUNK])
@@ -352,18 +353,19 @@ def tile_gaussianrenderer_kernel(tc, xyzs, latents, W1, b1, W2, b2, out):
         def end_of_chunks():
             nc.vector.tensor_copy(out=out_sb[:, :, 2 * WIDTH : 2 * WIDTH + 1], in_=addend[:, 0, :, ROWS : ROWS + 1])
 
-        def means(k):
+        def means(k, first=0, count=ROWS):
+            rows = slice(first, first + count)
             nc.vector.scalar_tensor_tensor(
-                out=out_sb[:, k, 0 : 2 * WIDTH].rearrange("p (r c) -> p r c", c=CH)[:, :, 0:4],
-                in0=tanh_back(k, slice(0, 4)), scalar=0.1,
-                in1=addend[:, :, k, 0:ROWS].rearrange("p s r -> p r s"), op0=ALU.mult, op1=ALU.add,
+                out=out_sb[:, k, 0 : 2 * WIDTH].rearrange("p (r c) -> p r c", c=CH)[:, rows, 0:4],
+                in0=tanh_back(k, slice(0, 4))[:, rows], scalar=0.1,
+                in1=addend[:, :, k, rows].rearrange("p s r -> p r s"), op0=ALU.mult, op1=ALU.add,
             )
 
-        def opacity_and_sizes(k):
+        def opacity_and_sizes(k, first=0, count=ROWS):
+            rows = slice(first, first + count)
             nc.vector.scalar_tensor_tensor(
-                out=gaussians(k)[:, :, 3:7], in0=tanh_back(k, slice(4, 8)), scalar=1.0,
-                in1=half_scale[:].unsqueeze(1).to_broadcast([P, ROWS, 4]),
-                op0=ALU.add, op1=ALU.mult,
+                out=gaussians(k)[:, rows, 3:7], in0=tanh_back(k, slice(4, 8))[:, rows], scalar=1.0,
+                in1=half_scale[:].unsqueeze(1).to_broadcast([P, count, 4]), op0=ALU.add, op1=ALU.mult,
             )
 
         def rotations_and_store(k):
@@ -383,6 +385,10 @@ def tile_gaussianrenderer_kernel(tc, xyzs, latents, W1, b1, W2, b2, out):
                 in_=out_sb[:, k, LEAD : LEAD + 2 * WIDTH].rearrange("p (i f) -> p i f", i=2),
             )
 
+        def store_tile(i):
+            first = LEAD + (i % 2) * WIDTH
+            nc.sync.dma_start(out=out_v[:, i, :], in_=out_sb[:, i // 2, first : first + WIDTH])
+
         nc.vector.tensor_reduce(
             out=same_gauss[:], in_=ident[:].rearrange("p (j g) -> p g j", g=GAUSS), axis=mybir.AxisListType.X, op=ALU.add
         )
@@ -394,30 +400,34 @@ def tile_gaussianrenderer_kernel(tc, xyzs, latents, W1, b1, W2, b2, out):
         )
         nc.vector.tensor_copy(out=b2_rows[0:1, 2], in_=b2_by_channel[:, 7:11])
         nc.vector.tensor_copy(out=bias_rows[0:1].rearrange("o g c -> o (g c)"), in_=b_row[:, 1])
+        columns_of_biases()
+        spread_bias()
         keep_clock_up(3)
         regroup_w1_vector(0)
         regroup_w1_scalar(0)
-        quantise_w1(0)
+        spread = banks["bias"][:].rearrange("p (g c) -> p g c", c=CH)
+        nc.scalar.copy(out=bias_8[:], in_=spread[:, :, 7:15])
+        nc.scalar.copy(out=bias_15[:], in_=spread[:, :, 15])
+        nc.scalar.copy(out=bias_cols[:], in_=banks["bias cols"][:, 0 : GROUPS + 3])
+
         regroup_w1_vector(1)
         regroup_w1_scalar(1)
+        quantise_w1(0)
         transpose_latents(0)
-        copy_tile(1)
         quantise_w1(1)
         copy_tile(0)
+        copy_tile(1)
         transpose_latents(1)
-        columns_of_biases()
-        spread_bias()
         copy_tile(2)
         copy_tile(3)
-        nc.scalar.copy(out=bias_cols[:], in_=banks["bias cols"][:, 0 : GROUPS + 3])
-        spread = banks["bias"][:].rearrange("p (g c) -> p g c", c=CH)
         regroup_w2(11, 4, nc.scalar.copy)
         quantise_latents(0)
-        quantise_latents(1)
+
         regroup_w2(15, 1, nc.vector.tensor_copy)
         regroup_w2(0, 1, nc.vector.tensor_copy)
         for chan in range(1, 11, 2):
             regroup_w2(chan, 2, nc.vector.tensor_copy)
+        quantise_latents(1)
         layer1(0)
         silu(0)
         transpose_latents(2)
@@ -430,8 +440,6 @@ def tile_gaussianrenderer_kernel(tc, xyzs, latents, W1, b1, W2, b2, out):
         copy_tile(7)
         layer1(1)
         silu(1)
-        nc.scalar.copy(out=bias_8[:], in_=spread[:, :, 7:15])
-        nc.scalar.copy(out=bias_15[:], in_=spread[:, :, 15])
         regroup_h(0)
         quantise_latents(3)
         layer1(2)
@@ -448,6 +456,7 @@ def tile_gaussianrenderer_kernel(tc, xyzs, latents, W1, b1, W2, b2, out):
         regroup_h(2)
         quantise_h(1)
         layer2_tanh(1)
+        layer2_rest(1)
         layer2_rotations(1)
         sum_squares(0)
         turn_tanh(0)
@@ -455,47 +464,52 @@ def tile_gaussianrenderer_kernel(tc, xyzs, latents, W1, b1, W2, b2, out):
         tanh(1)
         quantise_h(2)
         regroup_h(3)
-        add_bias(0)
         layer2_rotations(2)
         sum_squares(1)
-        layer2_rest(1)
         squares(2)
         quantise_h(3)
+        add_bias(0)
         layer2_rotations(3)
-        sum_squares(2)
         squares(3)
-        turn_tanh(1)
-        opacity_and_sizes(0)
-        colours(0)
-        layer2_tanh(2)
         layer2_rest(2)
+        layer2_tanh(2)
+        tanh(2)
+        turn_tanh(1)
+        layer2_last_colour()
+        sum_squares(2)
         sum_squares(3)
         inverse_norms()
-        tanh(2)
-        layer2_last_colour()
+        opacity_and_sizes(0)
         add_bias(1)
+        colours(0)
+        add_bias(2)
+        opacity_and_sizes(1)
         layer2_tanh(3)
+        turn_tanh(2)
         layer2_rest(3)
         tanh(3)
-        opacity_and_sizes(1)
-        colours(1)
-        add_bias(2)
         add_bias_last_colour()
-        rotations(0)
+        colours(1)
+        colours(2)
         clip_last_colour()
-        rotations(1)
+        opacity_and_sizes(2)
+
         means(0)
         end_of_chunks()
+        rotations(0)
         store(0)
         means(1)
+        rotations(1)
         store(1)
-        add_bias(3)
-        colours(2)
+        means(2)
         rotations(2)
+        store(2)
+        add_bias(3)
         rotations(3)
         colours(3)
-        for k in (2, 3):
-            turn_tanh(k)
-            opacity_and_sizes(k)
-            means(k)
-            store(k)
+        turn_tanh(3)
+        opacity_and_sizes(3)
+        means(3, 0, 33)
+        store_tile(6)
+        means(3, 33, 31)
+        store_tile(7)

@@ -83,7 +83,7 @@ def tile_gaussianrenderer_kernel(tc, xyzs, latents, W1, b1, W2, b2, out):
         warm = keep.tile([P, 1], F32)
         nc.vector.memset(warm[:], 0.0)
         nc.scalar.activation(out=warm[:], in_=warm[:], func=ACT.Silu)
-        ones = keep.tile([P, P], BF16)
+        ones = keep.tile([P, WIDTH], BF16)
         nc.vector.memset(ones[:], 1.0)
         ident = keep.tile([P, P], F32)
         make_identity(nc, ident[:])
@@ -171,7 +171,7 @@ def tile_gaussianrenderer_kernel(tc, xyzs, latents, W1, b1, W2, b2, out):
         def spread_bias():
             bank = bank_tile("bias", "G", [P, WIDTH])
             nc.tensor.matmul(
-                out=bank[:], lhsT=ones[:], rhs=bias_rows[:].rearrange("p g c -> p (g c)"),
+                out=bank[:], lhsT=ones[:, 0:P], rhs=bias_rows[:].rearrange("p g c -> p (g c)"),
                 start=True, stop=True,
             )
 
@@ -185,10 +185,17 @@ def tile_gaussianrenderer_kernel(tc, xyzs, latents, W1, b1, W2, b2, out):
                 )
 
         def keep_clock_up(count):
-            if "idle" not in banks:
-                bank_tile("idle", "A", [P, WIDTH])
+            bank = bank_tile("idle", "A", [P, WIDTH])
             for j in range(count):
-                nc.tensor.matmul(out=banks["idle"][:], lhsT=ones[:], rhs=w1_raw[:, 0, 0:WIDTH], start=True, stop=True)
+                nc.tensor.matmul(out=bank[:], lhsT=ones[:, 0:P], rhs=ones[:], start=True, stop=True)
+
+        def keep_clock_up_mx(count):
+            bank = bank_tile("idle", "A", [P, WIDTH])
+            for j in range(count):
+                nc.tensor.matmul_mx(
+                    out=bank[:], lhsT=w1_codes[:, 0, 0:P].bitcast(FP8X4), lhsT_scale=w1_scales[:, 0, 0:P],
+                    rhs=w1_codes[:, 0, :].bitcast(FP8X4), rhs_scale=w1_scales[:, 0, :], start=True, stop=True,
+                )
 
         def transpose_latents(k):
             for i in range(2):
@@ -400,6 +407,7 @@ def tile_gaussianrenderer_kernel(tc, xyzs, latents, W1, b1, W2, b2, out):
         )
         nc.vector.tensor_copy(out=b2_rows[0:1, 2], in_=b2_by_channel[:, 7:11])
         nc.vector.tensor_copy(out=bias_rows[0:1].rearrange("o g c -> o (g c)"), in_=b_row[:, 1])
+        keep_clock_up(3)
         columns_of_biases()
         spread_bias()
         keep_clock_up(3)
@@ -414,10 +422,12 @@ def tile_gaussianrenderer_kernel(tc, xyzs, latents, W1, b1, W2, b2, out):
         regroup_w1_scalar(1)
         quantise_w1(0)
         transpose_latents(0)
+        keep_clock_up_mx(2)
         quantise_w1(1)
         copy_tile(0)
         copy_tile(1)
         transpose_latents(1)
+        keep_clock_up_mx(2)
         copy_tile(2)
         copy_tile(3)
         regroup_w2(11, 4, nc.scalar.copy)
@@ -509,7 +519,5 @@ def tile_gaussianrenderer_kernel(tc, xyzs, latents, W1, b1, W2, b2, out):
         colours(3)
         turn_tanh(3)
         opacity_and_sizes(3)
-        means(3, 0, 33)
-        store_tile(6)
-        means(3, 33, 31)
-        store_tile(7)
+        means(3)
+        store(3)

@@ -26,10 +26,9 @@ W1_VECTOR_COLS = 384
 LEAD = 1
 VLAT = (5, 7)
 BL = "CDEFCDEF"
-BT = "EFCE"
-BF_ = "CDFD"
-BB = "ABFA"
-BR = "GGGE"
+BT = "DFBC"
+BF_ = "EAEA"
+BB = "DFBC"
 
 FLOPS = 2 * TOKENS * K1 * WIDTH + 2 * TOKENS * WIDTH * WIDTH
 
@@ -277,7 +276,11 @@ def tile_gaussianrenderer_kernel(tc, xyzs, latents, W1, b1, W2, b2, out):
             )
 
         def layer2_rotations(k):
-            layer2_transposed(k, 2, bank_tile(("rot", k), BR[k], [P, CHUNK])[:])
+            if k == 3:
+                banks[("rot", k)] = banks["norm"][:, CHUNKS * ROWS :]
+            else:
+                banks[("rot", k)] = bank_tile(("rot bank", k), "CGC"[k], [P, CHUNK])[:]
+            layer2_transposed(k, 2, banks[("rot", k)])
 
         def layer2_tanh(k):
             bank = bank_tile(("tanh", k), BT[k], [P, 2, CHUNK])
@@ -303,13 +306,13 @@ def tile_gaussianrenderer_kernel(tc, xyzs, latents, W1, b1, W2, b2, out):
 
         def squares(k):
             nc.scalar.activation(
-                out=squares_t[k][:], in_=banks[("rot", k)][:],
+                out=squares_t[k][:], in_=banks[("rot", k)],
                 func=ACT.Square, bias=bias_cols[:, GROUPS + 2 : GROUPS + 3], scale=1.0,
             )
 
         def sum_squares(k):
             if k == 0:
-                bank_tile("norm", "N", [P, CHUNKS * ROWS])
+                bank_tile("norm", "N", [P, WIDTH])
             for i in range(2):
                 first = (2 * k + i) * GAUSS
                 nc.tensor.matmul(
@@ -342,7 +345,7 @@ def tile_gaussianrenderer_kernel(tc, xyzs, latents, W1, b1, W2, b2, out):
             )
 
         def inverse_norms():
-            nc.scalar.activation(out=inv_norm[:], in_=banks["norm"][:], func=ACT.Abs_reciprocal_sqrt)
+            nc.scalar.activation(out=inv_norm[:], in_=banks["norm"][:, 0 : CHUNKS * ROWS], func=ACT.Abs_reciprocal_sqrt)
 
         def colours(k):
             nc.vector.tensor_scalar(
@@ -465,44 +468,45 @@ def tile_gaussianrenderer_kernel(tc, xyzs, latents, W1, b1, W2, b2, out):
         tanh(0)
         regroup_h(2)
         quantise_h(1)
+        layer2_rotations(1)
         layer2_tanh(1)
         layer2_rest(1)
-        layer2_rotations(1)
-        sum_squares(0)
-        turn_tanh(0)
         squares(1)
         tanh(1)
         quantise_h(2)
         regroup_h(3)
         layer2_rotations(2)
-        sum_squares(1)
+        layer2_tanh(2)
         squares(2)
         quantise_h(3)
         add_bias(0)
+        sum_squares(0)
+        sum_squares(1)
         layer2_rotations(3)
         squares(3)
+
         layer2_rest(2)
-        layer2_tanh(2)
+        turn_tanh(0)
         tanh(2)
-        turn_tanh(1)
-        layer2_last_colour()
         sum_squares(2)
+        layer2_last_colour()
         sum_squares(3)
+        turn_tanh(1)
         inverse_norms()
-        opacity_and_sizes(0)
         add_bias(1)
+        opacity_and_sizes(0)
         colours(0)
         add_bias(2)
-        opacity_and_sizes(1)
-        layer2_tanh(3)
-        turn_tanh(2)
-        layer2_rest(3)
-        tanh(3)
-        add_bias_last_colour()
         colours(1)
+        add_bias_last_colour()
+
         colours(2)
         clip_last_colour()
-        opacity_and_sizes(2)
+        opacity_and_sizes(1)
+        layer2_tanh(3)
+        layer2_rest(3)
+        turn_tanh(2)
+        tanh(3)
 
         means(0)
         end_of_chunks()
@@ -511,12 +515,16 @@ def tile_gaussianrenderer_kernel(tc, xyzs, latents, W1, b1, W2, b2, out):
         means(1)
         rotations(1)
         store(1)
+        opacity_and_sizes(2)
         means(2)
         rotations(2)
         store(2)
         add_bias(3)
-        rotations(3)
+
+
         colours(3)
+        rotations(3)
+
         turn_tanh(3)
         opacity_and_sizes(3)
         means(3)

@@ -24,7 +24,7 @@ ROWS = 2 * GAUSS
 GROUPS = WIDTH // P
 W1_VECTOR_COLS = 384
 LEAD = 1
-VLAT = (5, 7)
+VLAT = (4, 6)
 BL = "CDEFCDEF"
 BT = "DFBC"
 BF_ = "EAEA"
@@ -230,7 +230,7 @@ def tile_gaussianrenderer_kernel(tc, xyzs, latents, W1, b1, W2, b2, out):
         def layer1(k):
             for m in range(GROUPS):
                 if m % 2 == 0:
-                    bank_tile(("hT", k, m // 2), "AB"[m // 2], [P, 2, CHUNK])
+                    bank_tile(("hT", k, m // 2), "ABG"[(2 * k + m // 2) % 3], [P, 2, CHUNK])
                 cols = slice(m * P, (m + 1) * P)
                 for g in range(2):
                     toks = slice(g * CHUNK, (g + 1) * CHUNK)
@@ -445,10 +445,10 @@ def tile_gaussianrenderer_kernel(tc, xyzs, latents, W1, b1, W2, b2, out):
         silu(0)
         transpose_latents(2)
         transpose_latents(3)
+        quantise_w2()
         copy_tile(4)
         copy_tile(5)
         copy_tile(6)
-        quantise_w2()
         quantise_latents(2)
         copy_tile(7)
         layer1(1)

@@ -188,8 +188,8 @@ def tile_gaussianrenderer_kernel(tc, xyzs, latents, W1, b1, W2, b2, out):
             for j in range(count):
                 nc.tensor.matmul(out=bank[:], lhsT=ones[:, 0:P], rhs=ones[:], start=True, stop=True)
 
-        def keep_clock_up_mx(count):
-            bank = bank_tile("idle", "A", [P, WIDTH])
+        def keep_clock_up_mx(count, name="A"):
+            bank = bank_tile("idle", name, [P, WIDTH])
             for j in range(count):
                 nc.tensor.matmul_mx(
                     out=bank[:], lhsT=w1_codes[:, 0, 0:P].bitcast(FP8X4), lhsT_scale=w1_scales[:, 0, 0:P],
@@ -347,11 +347,9 @@ def tile_gaussianrenderer_kernel(tc, xyzs, latents, W1, b1, W2, b2, out):
         def inverse_norms():
             nc.scalar.activation(out=inv_norm[:], in_=banks["norm"][:, 0 : CHUNKS * ROWS], func=ACT.Abs_reciprocal_sqrt)
 
-        def colours(k):
-            nc.vector.tensor_scalar(
-                out=gaussians(k)[:, :, 11:15], in0=gaussians(k)[:, :, 11:15],
-                scalar1=0.0, scalar2=1.0, op0=ALU.max, op1=ALU.min,
-            )
+        def colours(first, count=1):
+            part = out_sb[:, first : first + count, LEAD : LEAD + 2 * WIDTH].rearrange("p k (r c) -> p k r c", c=CH)[..., 11:15]
+            nc.vector.tensor_scalar(out=part, in0=part, scalar1=0.0, scalar2=1.0, op0=ALU.max, op1=ALU.min)
 
         def clip_last_colour():
             last = addend[:, 0, :, 1 : ROWS + 1]
@@ -413,7 +411,7 @@ def tile_gaussianrenderer_kernel(tc, xyzs, latents, W1, b1, W2, b2, out):
         keep_clock_up(3)
         columns_of_biases()
         spread_bias()
-        keep_clock_up(3)
+        keep_clock_up(5)
         regroup_w1_vector(0)
         regroup_w1_scalar(0)
         spread = banks["bias"][:].rearrange("p (g c) -> p g c", c=CH)
@@ -495,9 +493,8 @@ def tile_gaussianrenderer_kernel(tc, xyzs, latents, W1, b1, W2, b2, out):
         inverse_norms()
         add_bias(1)
         opacity_and_sizes(0)
-        colours(0)
         add_bias(2)
-        colours(1)
+        colours(0, 2)
         add_bias_last_colour()
 
         colours(2)
@@ -517,14 +514,15 @@ def tile_gaussianrenderer_kernel(tc, xyzs, latents, W1, b1, W2, b2, out):
         store(1)
         opacity_and_sizes(2)
         means(2)
+        add_bias(3)
         rotations(2)
         store(2)
-        add_bias(3)
 
 
         colours(3)
         rotations(3)
 
+        keep_clock_up_mx(5, "G")
         turn_tanh(3)
         opacity_and_sizes(3)
         means(3)

@@ -22,7 +22,7 @@ CHUNKS = 4
 CHUNK = TOKENS // CHUNKS
 ROWS = 2 * GAUSS
 GROUPS = WIDTH // P
-W1_VECTOR_COLS = 384
+W1_VECTOR_COLS = 320
 LEAD = 1
 VLAT = (4, 6)
 BL = "CDEFCDEF"
@@ -435,9 +435,9 @@ def tile_gaussianrenderer_kernel(tc, xyzs, latents, W1, b1, W2, b2, out):
         quantise_latents(0)
 
         regroup_w2(15, 1, nc.vector.tensor_copy)
-        regroup_w2(0, 1, nc.vector.tensor_copy)
-        for chan in range(1, 11, 2):
-            regroup_w2(chan, 2, nc.vector.tensor_copy)
+        regroup_w2(0, 3, nc.vector.tensor_copy)
+        for chan in (3, 7):
+            regroup_w2(chan, 4, nc.vector.tensor_copy)
         quantise_latents(1)
         layer1(0)
         silu(0)
@@ -524,6 +524,9 @@ def tile_gaussianrenderer_kernel(tc, xyzs, latents, W1, b1, W2, b2, out):
 
         keep_clock_up_mx(5, "G")
         turn_tanh(3)
-        opacity_and_sizes(3)
-        means(3)
-        store(3)
+        opacity_and_sizes(3, 0, 32)
+        means(3, 0, 33)
+        store_tile(6)
+        opacity_and_sizes(3, 32, 32)
+        means(3, 33, 31)
+        store_tile(7)

from contextlib import ExitStack

import concourse.mybir as mybir
from concourse.masks import make_identity

FP8X4 = mybir.dt.float8_e4m3fn_x4
BF16 = mybir.dt.bfloat16
F32 = mybir.dt.float32
U32 = mybir.dt.uint32
U8 = mybir.dt.uint8
ACT = mybir.ActivationFunctionType
ALU = mybir.AluOpType

P = 128
TOKENS = 1024
K1 = 1024
WIDTH = 512
TILES = TOKENS // P
GAUSS = 32
CH = 16
CHUNKS = 4
CHUNK = TOKENS // CHUNKS
ROWS = 2 * GAUSS
GROUPS = WIDTH // P
W1_VECTOR_COLS = 320
LEAD = 1
VLAT = (4, 6)
BL = "CDEFCDEF"
BT = "DFBC"
BF_ = "EAEA"
BB = "DFBC"

FLOPS = 2 * TOKENS * K1 * WIDTH + 2 * TOKENS * WIDTH * WIDTH


def side_by_side(dst, src):
    return (
        dst.rearrange("p (c i) t -> p c t i", i=4),
        src.rearrange("p t (c i) -> p c t i", i=4),
    )


def tile_gaussianrenderer_kernel(tc, xyzs, latents, W1, b1, W2, b2, out):
    nc = tc.nc
    lat_v = latents.rearrange("b n d -> (b n) d").rearrange("(p i) d -> p i d", i=TILES)
    xyz_v = xyzs.rearrange("b n c -> (b n) c").rearrange("(p i) c -> p i c", i=TILES)
    out_v = out.rearrange("b (n g) c -> (b n) (g c)", g=GAUSS).rearrange("(p i) f -> p i f", i=TILES)
    w1_v = W1.rearrange("(a q e) c -> q a (e c)", a=4, e=2)
    w2_v = W2.rearrange("(t p) n -> p t n", p=P)

    with ExitStack() as ctx:
        ctx.enter_context(tc.manual_schedule())
        keep = ctx.enter_context(tc.tile_pool(name="keep", bufs=1))
        psum = ctx.enter_context(tc.psum_pool(name="psum", bufs=2))

        xyz_sb = keep.tile([P, TILES, 3], BF16)
        b1_rows = keep.tile([P, WIDTH], BF16)
        bias_rows = keep.tile([P, GAUSS, CH], BF16)
        b2_rows = keep.tile([P, 3, 4, GAUSS], BF16)
        w1_raw = keep.tile([P, 4, 2 * WIDTH], BF16)
        lat_sb = keep.tile([P, TILES, K1], BF16)
        w2_raw = keep.tile([P, 4, WIDTH], BF16)

        b_row = keep.tile([1, 2, WIDTH], BF16)
        nc.sync.dma_start(out=b_row[:, 0], in_=b1.unsqueeze(0))
        nc.sync.dma_start(out=b_row[:, 1], in_=b2.unsqueeze(0))
        nc.scalar.dma_start(out=xyz_sb[:], in_=xyz_v)
        nc.vector.memset(bias_rows[:].rearrange("p g c -> p (g c)").bitcast(U32), 0)
        nc.vector.memset(b1_rows[:].bitcast(U32), 0)
        nc.vector.memset(bias_rows[32:33, :, 11:16], 0.5)
        nc.vector.memset(b2_rows[:].rearrange("p a j g -> p (a j g)").bitcast(U32), 0)
        for g in range(2):
            nc.sync.dma_start(out=w1_raw[:, 2 * g : 2 * g + 2, :], in_=w1_v[:, 2 * g : 2 * g + 2, :])
        nc.sync.dma_start(out=lat_sb[:, 0, :], in_=lat_v[:, 0, :])
        nc.sync.dma_start(out=lat_sb[:, 1, :], in_=lat_v[:, 1, :])
        nc.sync.dma_start(out=lat_sb[:, 2, :], in_=lat_v[:, 2, :])
        nc.sync.dma_start(out=lat_sb[:, 3, :], in_=lat_v[:, 3, :])
        nc.sync.dma_start(out=w2_raw[:], in_=w2_v)
        nc.sync.dma_start(out=lat_sb[:, 4 : 6, :], in_=lat_v[:, 4 : 6, :])
        nc.sync.dma_start(out=lat_sb[:, 6 : 8, :], in_=lat_v[:, 6 : 8, :])

        warm = keep.tile([P, 1], F32)
        nc.vector.memset(warm[:], 0.0)
        nc.scalar.activation(out=warm[:], in_=warm[:], func=ACT.Silu)
        ones = keep.tile([P, WIDTH], BF16)
        nc.vector.memset(ones[:], 1.0)
        ident = keep.tile([P, P], F32)
        make_identity(nc, ident[:])
        half_scale = keep.tile([P, 4], F32)
        nc.gpsimd.memset(half_scale[:], 1.0)
        for cols, factor in ((slice(0, 1), 0.5), (slice(1, 4), 0.01)):
            nc.gpsimd.tensor_scalar(
                out=half_scale[:, cols], in0=half_scale[:, cols],
                scalar1=factor, scalar2=0.0, op0=ALU.mult, op1=ALU.add,
            )
        addend = keep.tile([P, 4, CHUNKS, ROWS + 2], F32)
        nc.gpsimd.memset(addend[:, 0, :, 0:1], 0.0)
        for c in range(3):
            nc.gpsimd.tensor_scalar(
                out=addend[:, 1 + c, :, 0:ROWS].rearrange("p k (i g) -> p k i g", g=GAUSS),
                in0=xyz_sb[:, :, c].rearrange("p (k i) -> p k i", i=2).unsqueeze(3).to_broadcast([P, CHUNKS, 2, GAUSS]),
                scalar1=1.0, scalar2=0.1, op0=ALU.mult, op1=ALU.add,
            )
        half_cols = keep.tile([P, 2], F32)
        nc.gpsimd.memset(half_cols[:], 0.5)
        nc.gpsimd.memset(half_cols[0:GAUSS, 0:1], 0.0)

        bias_cols = keep.tile([P, GROUPS + 3], F32)
        bias_8 = keep.tile([P, GAUSS, 8], F32)
        bias_15 = keep.tile([P, GAUSS], F32)
        same_gauss = keep.tile([P, GAUSS], F32)
        w1_grouped = [keep.tile([P, WIDTH, 4], BF16, align_bytes=64, name="w1_grouped%d" % g) for g in range(2)]
        w1_codes = keep.tile([P, 2, WIDTH], U32, align_bytes=64)
        w1_scales = keep.tile([P, 2, WIDTH], U8, align_bytes=64)
        w2_grouped = keep.tile([P, WIDTH, 4], BF16, align_bytes=64)
        w2_codes = keep.tile([P, WIDTH], U32, align_bytes=64)
        w2_scales = keep.tile([P, WIDTH], U8, align_bytes=64)
        lat_grouped = [keep.tile([P, 8 * CHUNK], BF16, align_bytes=64, name="lat_grouped%d" % k) for k in range(CHUNKS)]
        lat_codes = keep.tile([P, CHUNKS, 2 * CHUNK], U32, align_bytes=64)
        lat_scales = keep.tile([P, CHUNKS, 2 * CHUNK], U8, align_bytes=64)
        h_planes = [keep.tile([P, GROUPS, CHUNK], BF16, name="h_planes%d" % k) for k in range(CHUNKS)]
        h_grouped = [keep.tile([P, CHUNK, 4], BF16, align_bytes=64, name="h_grouped%d" % k) for k in range(CHUNKS)]
        h_codes = keep.tile([P, CHUNKS, CHUNK], U32, align_bytes=64)
        h_scales = keep.tile([P, CHUNKS, CHUNK], U8, align_bytes=64)
        out_sb = keep.tile([P, CHUNKS, 2 * WIDTH + 4], F32)
        tanh_t = [keep.tile([P, 2, CHUNK], F32, name="tanh_t%d" % k) for k in range(CHUNKS)]
        squares_t = [keep.tile([P, CHUNK], F32, name="squares_t%d" % k) for k in range(CHUNKS)]
        last_colour = keep.tile([P, TILES, GAUSS], F32)
        inv_norm = keep.tile([P, CHUNKS * ROWS], F32)
        banks = {}

        def channels(k):
            return out_sb[:, k, LEAD : LEAD + 2 * WIDTH].rearrange("p (i g c) -> p i g c", i=2, c=CH)

        def gaussians(k):
            return out_sb[:, k, LEAD : LEAD + 2 * WIDTH].rearrange("p (r c) -> p r c", c=CH)

        def bank_tile(key, bank, shape):
            banks[key] = psum.tile(shape, F32, tag=bank, bufs=1, name="bank%s" % bank)
            return banks[key]

        def w1_rows(g):
            return w1_raw[:, 2 * g : 2 * g + 2, :].rearrange("p u (e c) -> p (u e) c", e=2)

        def regroup_w1_vector(g):
            dst, src = side_by_side(w1_grouped[g][:, 0:W1_VECTOR_COLS, :], w1_rows(g)[:, :, 0:W1_VECTOR_COLS])
            nc.vector.tensor_copy(out=dst, in_=src)

        def regroup_w1_scalar(g):
            dst, src = side_by_side(w1_grouped[g][:, W1_VECTOR_COLS:, :], w1_rows(g)[:, :, W1_VECTOR_COLS:])
            nc.scalar.copy(out=dst, in_=src)

        def quantise_w1(g):
            nc.vector.quantize_mx(
                out=w1_codes[:, g, :].bitcast(FP8X4), scales=w1_scales[:, g, :],
                in_=w1_grouped[g][:].rearrange("p c t -> p (c t)"),
            )

        def regroup_w2(chan, count, copy):
            first = (chan + 1) % CH
            dst = w2_grouped[:].rearrange("p (s g) t -> p g s t", g=GAUSS)
            src = w2_raw[:].rearrange("p t (g c) -> p g c t", c=CH)
            copy(out=dst[:, :, first : first + count], in_=src[:, :, chan : chan + count])

        def quantise_w2():
            nc.vector.quantize_mx(
                out=w2_codes[:].bitcast(FP8X4), scales=w2_scales[:], in_=w2_grouped[:].rearrange("p c t -> p (c t)")
            )

        def spread_bias():
            bank = bank_tile("bias", "G", [P, WIDTH])
            nc.tensor.matmul(
                out=bank[:], lhsT=ones[:, 0:P], rhs=bias_rows[:].rearrange("p g c -> p (g c)"),
                start=True, stop=True,
            )

        def columns_of_biases():
            bank = bank_tile("bias cols", "N", [P, WIDTH])
            b2_cols = b2_rows[:].rearrange("p a j g -> p (a j g)")
            for m in range(GROUPS + 3):
                rows, first = (b1_rows[:], m * P) if m < GROUPS else (b2_cols, (m - GROUPS) * P)
                nc.tensor.matmul(
                    out=bank[:, m : m + 1], lhsT=rows[:, first : first + P], rhs=ones[:, 0:1], start=True, stop=True
                )

        def keep_clock_up(count):
            bank = bank_tile("idle", "A", [P, WIDTH])
            for j in range(count):
                nc.tensor.matmul(out=bank[:], lhsT=ones[:, 0:P], rhs=ones[:], start=True, stop=True)

        def keep_clock_up_mx(count, name="A"):
            bank = bank_tile("idle", name, [P, WIDTH])
            for j in range(count):
                nc.tensor.matmul_mx(
                    out=bank[:], lhsT=w1_codes[:, 0, 0:P].bitcast(FP8X4), lhsT_scale=w1_scales[:, 0, 0:P],
                    rhs=w1_codes[:, 0, :].bitcast(FP8X4), rhs_scale=w1_scales[:, 0, :], start=True, stop=True,
                )

        def transpose_latents(k):
            for i in range(2):
                transpose_tile(2 * k + i)

        def transpose_tile(i):
            bank = bank_tile(("latT", i), BL[i], [P, 2, 2, P])
            words = lat_sb[:, i, :].bitcast(F32)
            for g in range(2):
                for u in range(2):
                    first = 256 * g + 128 * u
                    nc.tensor.transpose(out=bank[:, g, u, :], in_=words[:, first : first + P], identity=ident[:])

        def copy_latents(k):
            for i in range(2):
                copy_tile(2 * k + i)

        def copy_tile(i):
            grouped = lat_grouped[i // 2][:].bitcast(F32).rearrange("p (g n u) -> p g n u", g=2, u=2)
            toks = slice((i % 2) * P, (i % 2 + 1) * P)
            out = grouped[:, :, toks]
            src = banks[("latT", i)][:].rearrange("p g u n -> p g n u")
            if i in VLAT:
                nc.vector.tensor_copy(out=out, in_=src)
            else:
                nc.scalar.copy(out=out, in_=src)

        def quantise_latents(k):
            nc.vector.quantize_mx(
                out=lat_codes[:, k, :].bitcast(FP8X4), scales=lat_scales[:, k, :], in_=lat_grouped[k][:]
            )

        def layer1(k):
            for m in range(GROUPS):
                if m % 2 == 0:
                    bank_tile(("hT", k, m // 2), "ABG"[(2 * k + m // 2) % 3], [P, 2, CHUNK])
                cols = slice(m * P, (m + 1) * P)
                for g in range(2):
                    toks = slice(g * CHUNK, (g + 1) * CHUNK)
                    nc.tensor.matmul_mx(
                        out=banks[("hT", k, m // 2)][:, m % 2, :],
                        lhsT=w1_codes[:, g, cols].bitcast(FP8X4),
                        lhsT_scale=w1_scales[:, g, cols],
                        rhs=lat_codes[:, k, toks].bitcast(FP8X4),
                        rhs_scale=lat_scales[:, k, toks],
                        start=(g == 0),
                        stop=(g == 1),
                    )

        def silu(k):
            for m in range(GROUPS):
                nc.scalar.activation(
                    out=h_planes[k][:, m, :], in_=banks[("hT", k, m // 2)][:, m % 2, :],
                    func=ACT.Silu, bias=bias_cols[:, m : m + 1], scale=1.0,
                )

        def regroup_h(k):
            dst, src = side_by_side(h_grouped[k][:], h_planes[k][:])
            nc.vector.tensor_copy(out=dst, in_=src)

        def quantise_h(k):
            nc.vector.quantize_mx(
                out=h_codes[:, k, :].bitcast(FP8X4), scales=h_scales[:, k, :],
                in_=h_grouped[k][:].rearrange("p n t -> p (n t)"),
            )

        def layer2_transposed(k, a, out):
            cols = slice(a * P, (a + 1) * P)
            nc.tensor.matmul_mx(
                out=out, lhsT=w2_codes[:, cols].bitcast(FP8X4), lhsT_scale=w2_scales[:, cols],
                rhs=h_codes[:, k, :].bitcast(FP8X4), rhs_scale=h_scales[:, k, :], start=True, stop=True,
            )

        def layer2_tokens(i, cols, out):
            toks = slice((i % 2) * P, (i % 2 + 1) * P)
            nc.tensor.matmul_mx(
                out=out, lhsT=h_codes[:, i // 2, toks].bitcast(FP8X4), lhsT_scale=h_scales[:, i // 2, toks],
                rhs=w2_codes[:, cols].bitcast(FP8X4), rhs_scale=w2_scales[:, cols], start=True, stop=True,
            )

        def layer2_rotations(k):
            if k == 3:
                banks[("rot", k)] = banks["norm"][:, CHUNKS * ROWS :]
            else:
                banks[("rot", k)] = bank_tile(("rot bank", k), "CGC"[k], [P, CHUNK])[:]
            layer2_transposed(k, 2, banks[("rot", k)])

        def layer2_tanh(k):
            bank = bank_tile(("tanh", k), BT[k], [P, 2, CHUNK])
            for a in range(2):
                layer2_transposed(k, a, bank[:, a, :])

        def layer2_rest(k):
            bank = bank_tile(("f", k), BF_[k], [P, 2, 2 * P])
            for i in range(2):
                layer2_tokens(2 * k + i, slice(2 * P, 4 * P), bank[:, i, :])

        def layer2_last_colour():
            bank = bank_tile("last", "G", [P, TILES, 64])
            for i in range(TILES):
                layer2_tokens(i, slice(0, 64), bank[:, i, :])

        def tanh(k):
            for a in range(2):
                nc.scalar.activation(
                    out=tanh_t[k][:, a, :], in_=banks[("tanh", k)][:, a, :],
                    func=ACT.Tanh, bias=bias_cols[:, GROUPS + a : GROUPS + a + 1], scale=half_cols[:, a : a + 1],
                )

        def squares(k):
            nc.scalar.activation(
                out=squares_t[k][:], in_=banks[("rot", k)],
                func=ACT.Square, bias=bias_cols[:, GROUPS + 2 : GROUPS + 3], scale=1.0,
            )

        def sum_squares(k):
            if k == 0:
                bank_tile("norm", "N", [P, WIDTH])
            for i in range(2):
                first = (2 * k + i) * GAUSS
                nc.tensor.matmul(
                    out=banks["norm"][:, first : first + GAUSS], lhsT=squares_t[k][:, i * P : (i + 1) * P],
                    rhs=same_gauss[:], start=True, stop=True,
                )

        def turn_tanh(k):
            bank = bank_tile(("tanh back", k), BB[k], [P, 8, 2, GAUSS])
            for i in range(2):
                for a in range(2):
                    nc.tensor.transpose(
                        out=bank[:, 4 * a : 4 * a + 4, i, :], in_=tanh_t[k][:, a, i * P : (i + 1) * P], identity=ident[:]
                    )

        def tanh_back(k, slots):
            return banks[("tanh back", k)][:, slots].rearrange("p s i g -> p (i g) s")

        def add_bias(k):
            nc.vector.tensor_tensor(
                out=channels(k)[:, :, :, 7:15],
                in0=banks[("f", k)][:].rearrange("p i (s g) -> p i g s", g=GAUSS),
                in1=bias_8[:].unsqueeze(1).to_broadcast([P, 2, GAUSS, 8]), op=ALU.add,
            )

        def add_bias_last_colour():
            nc.vector.tensor_tensor(
                out=last_colour[:], in0=banks["last"][:, :, 0:GAUSS],
                in1=bias_15[:].unsqueeze(1).to_broadcast([P, TILES, GAUSS]), op=ALU.add,
            )

        def inverse_norms():
            nc.scalar.activation(out=inv_norm[:], in_=banks["norm"][:, 0 : CHUNKS * ROWS], func=ACT.Abs_reciprocal_sqrt)

        def colours(first, count=1):
            part = out_sb[:, first : first + count, LEAD : LEAD + 2 * WIDTH].rearrange("p k (r c) -> p k r c", c=CH)[..., 11:15]
            nc.vector.tensor_scalar(out=part, in0=part, scalar1=0.0, scalar2=1.0, op0=ALU.max, op1=ALU.min)

        def clip_last_colour():
            last = addend[:, 0, :, 1 : ROWS + 1]
            nc.vector.tensor_scalar(
                out=last, in0=last_colour[:].rearrange("p (k i) g -> p k (i g)", i=2),
                scalar1=0.0, scalar2=1.0, op0=ALU.max, op1=ALU.min,
            )

        def end_of_chunks():
            nc.vector.tensor_copy(out=out_sb[:, :, 2 * WIDTH : 2 * WIDTH + 1], in_=addend[:, 0, :, ROWS : ROWS + 1])

        def means(k, first=0, count=ROWS):
            rows = slice(first, first + count)
            nc.vector.scalar_tensor_tensor(
                out=out_sb[:, k, 0 : 2 * WIDTH].rearrange("p (r c) -> p r c", c=CH)[:, rows, 0:4],
                in0=tanh_back(k, slice(0, 4))[:, rows], scalar=0.1,
                in1=addend[:, :, k, rows].rearrange("p s r -> p r s"), op0=ALU.mult, op1=ALU.add,
            )

        def opacity_and_sizes(k, first=0, count=ROWS):
            rows = slice(first, first + count)
            nc.vector.scalar_tensor_tensor(
                out=gaussians(k)[:, rows, 3:7], in0=tanh_back(k, slice(4, 8))[:, rows], scalar=1.0,
                in1=half_scale[:].unsqueeze(1).to_broadcast([P, count, 4]), op0=ALU.add, op1=ALU.mult,
            )

        def rotations_and_store(k):
            rotations(k)
            store(k)

        def rotations(k):
            inverse = inv_norm[:, k * ROWS : (k + 1) * ROWS]
            nc.vector.scalar_tensor_tensor(
                out=gaussians(k)[:, :, 7:11], in0=inverse.unsqueeze(2).to_broadcast([P, ROWS, 4]),
                scalar=1e12, in1=gaussians(k)[:, :, 7:11], op0=ALU.min, op1=ALU.mult,
            )

        def store(k):
            nc.sync.dma_start(
                out=out_v[:, 2 * k : 2 * k + 2, :],
                in_=out_sb[:, k, LEAD : LEAD + 2 * WIDTH].rearrange("p (i f) -> p i f", i=2),
            )

        def store_tile(i):
            first = LEAD + (i % 2) * WIDTH
            nc.sync.dma_start(out=out_v[:, i, :], in_=out_sb[:, i // 2, first : first + WIDTH])

        nc.vector.tensor_reduce(
            out=same_gauss[:], in_=ident[:].rearrange("p (j g) -> p g j", g=GAUSS), axis=mybir.AxisListType.X, op=ALU.add
        )
        b2_by_channel = b_row[:, 1].rearrange("o (g c) -> o c g", c=CH)
        nc.vector.tensor_copy(out=b1_rows[0:1], in_=b_row[:, 0])
        nc.vector.tensor_scalar(
            out=b2_rows[0:1].rearrange("o a j g -> o (a j) g")[:, 1:8], in0=b2_by_channel[:, 0:7],
            scalar1=0.5, scalar2=0.0, op0=ALU.mult, op1=ALU.add,
        )
        nc.vector.tensor_copy(out=b2_rows[0:1, 2], in_=b2_by_channel[:, 7:11])
        nc.vector.tensor_copy(out=bias_rows[0:1].rearrange("o g c -> o (g c)"), in_=b_row[:, 1])
        keep_clock_up(3)
        columns_of_biases()
        spread_bias()
        keep_clock_up(5)
        regroup_w1_vector(0)
        regroup_w1_scalar(0)
        spread = banks["bias"][:].rearrange("p (g c) -> p g c", c=CH)
        nc.scalar.copy(out=bias_8[:], in_=spread[:, :, 7:15])
        nc.scalar.copy(out=bias_15[:], in_=spread[:, :, 15])
        nc.scalar.copy(out=bias_cols[:], in_=banks["bias cols"][:, 0 : GROUPS + 3])

        regroup_w1_vector(1)
        regroup_w1_scalar(1)
        quantise_w1(0)
        transpose_latents(0)
        keep_clock_up_mx(2)
        quantise_w1(1)
        copy_tile(0)
        copy_tile(1)
        transpose_latents(1)
        keep_clock_up_mx(2)
        copy_tile(2)
        copy_tile(3)
        regroup_w2(11, 4, nc.scalar.copy)
        quantise_latents(0)

        regroup_w2(15, 1, nc.vector.tensor_copy)
        regroup_w2(0, 3, nc.vector.tensor_copy)
        for chan in (3, 7):
            regroup_w2(chan, 4, nc.vector.tensor_copy)
        quantise_latents(1)
        layer1(0)
        silu(0)
        transpose_latents(2)
        transpose_latents(3)
        quantise_w2()
        copy_tile(4)
        copy_tile(5)
        copy_tile(6)
        quantise_latents(2)
        copy_tile(7)
        layer1(1)
        silu(1)
        regroup_h(0)
        quantise_latents(3)
        layer1(2)
        silu(2)
        regroup_h(1)
        quantise_h(0)
        layer1(3)
        silu(3)
        layer2_rotations(0)
        layer2_tanh(0)
        layer2_rest(0)
        squares(0)
        tanh(0)
        regroup_h(2)
        quantise_h(1)
        layer2_rotations(1)
        layer2_tanh(1)
        layer2_rest(1)
        squares(1)
        tanh(1)
        quantise_h(2)
        regroup_h(3)
        layer2_rotations(2)
        layer2_tanh(2)
        squares(2)
        quantise_h(3)
        add_bias(0)
        sum_squares(0)
        sum_squares(1)
        layer2_rotations(3)
        squares(3)

        layer2_rest(2)
        turn_tanh(0)
        tanh(2)
        sum_squares(2)
        layer2_last_colour()
        sum_squares(3)
        turn_tanh(1)
        inverse_norms()
        add_bias(1)
        opacity_and_sizes(0)
        add_bias(2)
        colours(0, 2)
        add_bias_last_colour()

        colours(2)
        clip_last_colour()
        opacity_and_sizes(1)
        layer2_tanh(3)
        layer2_rest(3)
        turn_tanh(2)
        tanh(3)

        means(0)
        end_of_chunks()
        rotations(0)
        store(0)
        means(1)
        rotations(1)
        store(1)
        opacity_and_sizes(2)
        means(2)
        add_bias(3)
        rotations(2)
        store(2)


        colours(3)
        rotations(3)

        keep_clock_up_mx(5, "G")
        turn_tanh(3)
        opacity_and_sizes(3, 0, 32)
        means(3, 0, 33)
        store_tile(6)
        opacity_and_sizes(3, 32, 32)
        means(3, 33, 31)
        store_tile(7)
